import numpy as np
import ml_dtypes


def mxq(x, axis, fmt="e4m3"):
    dtype, down = {"e4m3": (ml_dtypes.float8_e4m3fn, 7), "e5m2": (ml_dtypes.float8_e5m2, 14)}[fmt]
    v = np.moveaxis(np.asarray(x, np.float32).astype(ml_dtypes.bfloat16).astype(np.float64), axis, -1)
    blocks = v.reshape(v.shape[:-1] + (-1, 32))
    amax = np.abs(blocks).max(-1, keepdims=True)
    byte = np.maximum(np.where(amax > 0, np.frexp(amax)[1] - 1 + 127, 0) - down, 1)
    scale = np.exp2(byte - 127.0)
    codes = (blocks / scale).astype(np.float32).astype(dtype).astype(np.float64)
    return np.moveaxis((codes * scale).reshape(v.shape), -1, axis)


WIDE = False


def mx_kscale(k):
    if not WIDE:
        return np.ones(k)
    levels = np.array([10, -10, 5, -5, 0])
    a = np.random.permutation(np.resize(levels, k // 512 * 4)).reshape(k // 512, 4)
    idx = np.arange(k)
    return np.exp2(a[idx // 512, idx % 128 // 32])


BF16 = ml_dtypes.bfloat16


def bf(x):
    return np.asarray(x, np.float32).astype(BF16)


def f64(x):
    return np.asarray(x).astype(np.float64)


B, C, V, K, OUT = 16, 128, 1024, 4, 128


def setup_inputs():
    a = mx_kscale(C * K)[::K]
    ab = np.repeat(a, B)
    ak = np.repeat(a, K)
    g = np.random.standard_normal((V, V))
    lap = (g + g.T) * (0.45 / np.sqrt(V))
    return {"input": bf(np.random.standard_normal((B, C, V)) * a[None, :, None]),
            "x1": bf(np.random.standard_normal((V, C * B)) * 0.64 * ab),
            "x2": bf(np.random.standard_normal((V, C * B)) * 0.83 * ab),
            "laplacian": bf(lap),
            "weight": bf(np.random.standard_normal((OUT, C * K)) / np.sqrt(C * K) / ak),
            "bias": bf(np.random.standard_normal(OUT) * 0.2)}


def reference(input, x1, x2, laplacian, weight, bias):
    x0 = f64(input).transpose(2, 1, 0).reshape(V, C * B)
    x1 = f64(x1)
    x2 = f64(x2)
    x3 = 2.0 * (mxq(f64(laplacian), 1, "e4m3") @ mxq(x2, 0, "e4m3")) - x1
    x = np.stack([x0, x1, x2, x3], axis=0)
    x = x.reshape(K, V, C, B)
    x = x.transpose(3, 1, 2, 0)
    x = x.reshape(B * V, C * K)
    y = (mxq(x, 1, "e4m3") @ mxq(f64(weight), 1, "e4m3").T) + f64(bias)
    y = y.reshape(B, V, OUT)
    return y.transpose(0, 2, 1)

@@ -1,0 +1,236 @@
+from contextlib import ExitStack
+
+import concourse.mybir as mybir
+from concourse.masks import make_identity
+
+F32 = mybir.dt.float32
+BF16 = mybir.dt.bfloat16
+U32 = mybir.dt.uint32
+U8 = mybir.dt.uint8
+FP8X4 = mybir.dt.float8_e4m3fn_x4
+ALU = mybir.AluOpType
+ACT = mybir.ActivationFunctionType
+
+P = 128
+B, C, V, K, OUT = 16, 128, 1024, 4, 128
+VB = 256
+NVB = V // VB
+UB = 8
+COLS = UB * VB
+FLOPS = 2 * V * V * C * B + 2 * B * V * C * K * OUT
+
+S_COLS = 192
+
+
+def tile_graph_conv_pb_t_kernel(tc, x0, x1, x2, laplacian, weight, bias, out):
+    nc = tc.nc
+    with ExitStack() as ctx:
+        const = ctx.enter_context(tc.tile_pool(name="const", bufs=1))
+        big = ctx.enter_context(tc.tile_pool(name="big", bufs=5))
+        chunk = ctx.enter_context(tc.tile_pool(name="chunk", bufs=2))
+        x0_pool = ctx.enter_context(tc.tile_pool(name="x0p", bufs=3))
+        f_pool = ctx.enter_context(tc.tile_pool(name="fp", bufs=2))
+        o_pool = ctx.enter_context(tc.tile_pool(name="op", bufs=2))
+        ps_t = ctx.enter_context(tc.psum_pool(name="pst", bufs=2))
+        ps_1 = ctx.enter_context(tc.psum_pool(name="ps1", bufs=3))
+        ps_2 = ctx.enter_context(tc.psum_pool(name="ps2", bufs=3))
+
+        ident = const.tile([P, P], F32)
+        make_identity(nc, ident[:])
+        ident_bf = const.tile([P, P], BF16)
+        make_identity(nc, ident_bf[:])
+
+        w_nat = const.tile([P, C * K], BF16)
+        nc.scalar.dma_start(out=w_nat[:], in_=weight)
+        bias_rows = const.tile([P, P], BF16)
+        nc.vector.memset(bias_rows[:], 0.0)
+        nc.scalar.dma_start(out=bias_rows[0:1, :], in_=bias.rearrange("(r o) -> r o", r=1))
+
+        x2n = const.tile([P, 8, C * B], BF16)
+        x2_words = x2n[:].bitcast(F32)
+
+        def load_x2(q):
+            nc.sync.dma_start(out=x2n[:, 2 * q:2 * q + 2, :],
+                              in_=x2[VB * q:VB * (q + 1), :].rearrange("(p e) n -> p e n", e=2))
+
+        l_tiles = {}
+        x1_tiles = {}
+        x0_tiles = {}
+
+        def load_l(q):
+            l_nat = chunk.tile([P, 2, V], BF16)
+            nc.sync.dma_start(out=l_nat[:], in_=laplacian[VB * q:VB * (q + 1), :].rearrange("(t p) u -> p t u", p=P))
+            l_tiles[q] = l_nat
+
+        def load_x1(q):
+            x1c = chunk.tile([P, 2, C * B], BF16)
+            nc.sync.dma_start(out=x1c[:], in_=x1[VB * q:VB * (q + 1), :].rearrange("(t p) n -> p t n", p=P))
+            x1_tiles[q] = x1c
+
+        def load_x0(q, bh):
+            x0n = x0_pool.tile([P, UB, VB], BF16)
+            nc.sync.dma_start(out=x0n[:],
+                              in_=x0[UB * bh:UB * (bh + 1), :, VB * q:VB * (q + 1)].rearrange("b c v -> c b v"))
+            x0_tiles[(q, bh)] = x0n
+
+        for q in range(4):
+            load_x2(q)
+        load_l(0)
+        load_x1(0)
+        load_x0(0, 0)
+        load_x0(0, 1)
+        load_l(1)
+        load_x1(1)
+        load_x0(1, 0)
+
+        w_words = w_nat[:].bitcast(F32)
+        w_ps = ps_t.tile([P, 2, P], F32, tag="tp")
+        for h in range(2):
+            nc.tensor.transpose(w_ps[:, h, :], w_words[:, h:2 * C:2], ident[:])
+        wg = const.tile([P, OUT, 4], BF16, align_bytes=64)
+        nc.scalar.copy(out=wg[:].bitcast(F32), in_=w_ps[:].rearrange("p h o -> p o h"))
+        w_codes = const.tile([P, OUT], U32, align_bytes=64)
+        w_sc = const.tile([P, OUT], U8, align_bytes=64)
+        nc.vector.quantize_mx(out=w_codes[:].bitcast(FP8X4), scales=w_sc[:],
+                              in_=wg[:].rearrange("p o t -> p (o t)"))
+        b_ps = ps_t.tile([P, P], BF16, tag="tp")
+        nc.tensor.transpose(b_ps[:], bias_rows[:], ident_bf[:])
+        bias_f = const.tile([P, 1], F32)
+        nc.vector.tensor_copy(out=bias_f[:], in_=b_ps[:, 0:1])
+
+        x2_codes = const.tile([P, 2, B * C], U32, align_bytes=64)
+        x2_sc = const.tile([P, 2, B * C], U8, align_bytes=64)
+        lt_codes = const.tile([P, 2, V], U32, align_bytes=64)
+        lt_sc = const.tile([P, 2, V], U8, align_bytes=64)
+
+        def prep_x2(g):
+            x2g = big.tile([P, B, C, 4], BF16, tag="big", align_bytes=64)
+            src = x2n[:, 4 * g:4 * g + 4, :].rearrange("p j (c b) -> p b c j", b=B)
+            for hq in range(2):
+                b0 = 8 * hq
+                nc.vector.tensor_copy(out=x2g[:, b0:b0 + 4], in_=src[:, b0:b0 + 4])
+                nc.scalar.copy(out=x2g[:, b0 + 6:b0 + 8], in_=src[:, b0 + 6:b0 + 8])
+                nc.vector.tensor_copy(out=x2g[:, b0 + 4:b0 + 6], in_=src[:, b0 + 4:b0 + 6])
+                cs = slice(hq * 1024, (hq + 1) * 1024)
+                nc.vector.quantize_mx(out=x2_codes[:, g, cs].bitcast(FP8X4), scales=x2_sc[:, g, cs],
+                                      in_=x2g[:, b0:b0 + 8].rearrange("p b c j -> p (b c j)"))
+
+        def prep_l(q):
+            l_words = l_tiles[q][:].bitcast(F32)
+            ltg = chunk.tile([P, 2, VB, 4], BF16, align_bytes=64)
+            ltg_words = ltg[:].bitcast(F32)
+            vs = slice(q * VB, (q + 1) * VB)
+            for g in range(2):
+                tp = ps_t.tile([P, 2, VB], F32, tag="tp")
+                for h in range(2):
+                    for tt in range(2):
+                        nc.tensor.transpose(tp[:, h, tt * P:(tt + 1) * P],
+                                            l_words[:, tt, 256 * g + 128 * h:256 * g + 128 * (h + 1)], ident[:])
+                nc.scalar.copy(out=ltg_words[:, g, :, :], in_=tp[:].rearrange("p h v -> p v h"))
+            for g in range(2):
+                nc.vector.quantize_mx(out=lt_codes[:, g, vs].bitcast(FP8X4), scales=lt_sc[:, g, vs],
+                                      in_=ltg[:, g, :, :].rearrange("p v t -> p (v t)"))
+
+        planes = {}
+        grouped = {}
+
+        def stage_a(q, bh):
+            xp = big.tile([P, K, COLS], BF16, tag="big", align_bytes=64)
+            planes[(q, bh)] = xp
+            xp_words = xp[:].bitcast(F32)
+            for lp in range(2):
+                tp = ps_t.tile([P, 2, 2, P], F32, tag="tp")
+                for l in range(2):
+                    bb = 4 * bh + 2 * lp + l
+                    for e in range(2):
+                        nc.tensor.transpose(tp[:, l, e, :], x2_words[:, 2 * q + e, bb:C * 8:8], ident[:])
+                nc.scalar.copy(out=xp_words[:, 2, lp * 512:(lp + 1) * 512].rearrange("p (l r e) -> p l r e", l=2, e=2),
+                               in_=tp[:].rearrange("p l e r -> p l r e"))
+            x1_words = x1_tiles[q][:].bitcast(F32)
+            for lp in range(2):
+                tp = ps_t.tile([P, 2, 2, P], F32, tag="tp")
+                for l in range(2):
+                    bb = 4 * bh + 2 * lp + l
+                    for tt in range(2):
+                        nc.tensor.transpose(tp[:, l, tt, :], x1_words[:, tt, bb:C * 8:8], ident[:])
+                nc.scalar.copy(out=xp_words[:, 1, lp * 512:(lp + 1) * 512],
+                               in_=tp[:].rearrange("p l t r -> p (l t r)"))
+            x0n = x0_tiles[(q, bh)]
+            nc.scalar.copy(out=xp[:, 0, :].rearrange("p (l v e) -> p l v e", l=4, e=2),
+                           in_=x0n[:].rearrange("p (l e) v -> p l v e", e=2))
+
+        def stage_b(q, bh):
+            xp = planes[(q, bh)]
+            vs = slice(q * VB, (q + 1) * VB)
+            for l in range(4):
+                m1 = ps_1.tile([P, 2, VB], F32, tag="m1")
+                for e in range(2):
+                    b = UB * bh + 2 * l + e
+                    bs = slice(b * C, (b + 1) * C)
+                    for g in range(2):
+                        nc.tensor.matmul_mx(out=m1[:, e, :],
+                                            lhsT=x2_codes[:, g, bs].bitcast(FP8X4), lhsT_scale=x2_sc[:, g, bs],
+                                            rhs=lt_codes[:, g, vs].bitcast(FP8X4), rhs_scale=lt_sc[:, g, vs],
+                                            start=(g == 0), stop=(g == 1))
+                ws = slice(l * 512, (l + 1) * 512)
+                nc.vector.scalar_tensor_tensor(out=xp[:, 3, ws], in0=m1[:].rearrange("p e v -> p v e"),
+                                               scalar=2.0, in1=xp[:, 1, ws],
+                                               op0=ALU.mult, op1=ALU.subtract)
+
+        def stage_c(q, bh):
+            xp = planes[(q, bh)]
+            fg = big.tile([P, COLS, K], BF16, tag="big", align_bytes=64)
+            f_codes = f_pool.tile([P, COLS], U32, align_bytes=64)
+            f_sc = f_pool.tile([P, COLS], U8, align_bytes=64)
+            grouped[(q, bh)] = (f_codes, f_sc)
+            for half in range(2):
+                a = half * 1024
+                m = a + 1024 - S_COLS
+                z = a + 1024
+                nc.vector.tensor_copy(out=fg[:, a:m, :].rearrange("p (c i) t -> p c t i", i=4),
+                                      in_=xp[:, :, a:m].rearrange("p t (c i) -> p c t i", i=4))
+                nc.scalar.copy(out=fg[:, m:z, :].rearrange("p (c i) t -> p c t i", i=4),
+                               in_=xp[:, :, m:z].rearrange("p t (c i) -> p c t i", i=4))
+            for half in range(2):
+                cs = slice(half * 1024, (half + 1) * 1024)
+                nc.vector.quantize_mx(out=f_codes[:, cs].bitcast(FP8X4), scales=f_sc[:, cs],
+                                      in_=fg[:, cs, :].rearrange("p w t -> p (w t)"))
+
+        def stage_d(q, bh):
+            f_codes, f_sc = grouped[(q, bh)]
+            o_sb = o_pool.tile([P, UB, VB], F32)
+            for l in range(4):
+                cs = slice(l * 512, (l + 1) * 512)
+                m2 = ps_2.tile([P, 512], F32, tag="m2")
+                nc.tensor.matmul_mx(out=m2[:], lhsT=w_codes[:].bitcast(FP8X4), lhsT_scale=w_sc[:],
+                                    rhs=f_codes[:, cs].bitcast(FP8X4), rhs_scale=f_sc[:, cs],
+                                    start=True, stop=True)
+                nc.scalar.activation(out=o_sb[:, 2 * l:2 * l + 2, :],
+                                     in_=m2[:].rearrange("p (v e) -> p e v", e=2),
+                                     func=ACT.Identity, bias=bias_f[:, 0:1], scale=1.0)
+            nc.scalar.dma_start(out=out[UB * bh:UB * (bh + 1), :, VB * q:VB * (q + 1)].rearrange("b o v -> o b v"),
+                                in_=o_sb[:])
+
+        units = [(q, bh) for q in range(NVB) for bh in range(2)]
+
+        prep_x2(0)
+        prep_l(0)
+        stage_a(0, 0)
+        prep_x2(1)
+        stage_a(0, 1)
+        for i in range(len(units)):
+            q, bh = units[i]
+            stage_b(q, bh)
+            if i + 2 < len(units):
+                q2, bh2 = units[i + 2]
+                if bh2 == 0:
+                    prep_l(q2)
+                    if q2 + 1 < NVB:
+                        load_l(q2 + 1)
+                        load_x1(q2 + 1)
+                stage_a(q2, bh2)
+                if i + 3 < len(units) and i + 3 >= 3:
+                    q3, bh3 = units[i + 3]
+                    load_x0(q3, bh3)
+            stage_c(q, bh)
+            stage_d(q, bh)

@@ -15,25 +15,31 @@ P = 128
 B, C, V, K, OUT = 16, 128, 1024, 4, 128
 VB = 256
 NVB = V // VB
-UB = 8
+UB = 4
+UPB = B // UB
+NU = NVB * UPB
 COLS = UB * VB
 FLOPS = 2 * V * V * C * B + 2 * B * V * C * K * OUT
 
 S_COLS = 192
+V_B = 10
+X0_AHEAD = 6
 
 
 def tile_graph_conv_pb_t_kernel(tc, x0, x1, x2, laplacian, weight, bias, out):
     nc = tc.nc
     with ExitStack() as ctx:
         const = ctx.enter_context(tc.tile_pool(name="const", bufs=1))
-        big = ctx.enter_context(tc.tile_pool(name="big", bufs=5))
+        x2g_pool = ctx.enter_context(tc.tile_pool(name="x2gp", bufs=2))
+        big = ctx.enter_context(tc.tile_pool(name="big", bufs=7))
         chunk = ctx.enter_context(tc.tile_pool(name="chunk", bufs=2))
-        x0_pool = ctx.enter_context(tc.tile_pool(name="x0p", bufs=3))
-        f_pool = ctx.enter_context(tc.tile_pool(name="fp", bufs=2))
-        o_pool = ctx.enter_context(tc.tile_pool(name="op", bufs=2))
+        x0_pool = ctx.enter_context(tc.tile_pool(name="x0p", bufs=X0_AHEAD))
+        f_pool = ctx.enter_context(tc.tile_pool(name="fp", bufs=3))
+        o_pool = ctx.enter_context(tc.tile_pool(name="op", bufs=4))
         ps_t = ctx.enter_context(tc.psum_pool(name="pst", bufs=2))
-        ps_1 = ctx.enter_context(tc.psum_pool(name="ps1", bufs=3))
-        ps_2 = ctx.enter_context(tc.psum_pool(name="ps2", bufs=3))
+        ps_1 = ctx.enter_context(tc.psum_pool(name="ps1", bufs=4))
+        ps_2 = ctx.enter_context(tc.psum_pool(name="ps2", bufs=2))
+        ctx.enter_context(tc.manual_schedule())
 
         ident = const.tile([P, P], F32)
         make_identity(nc, ident[:])
@@ -49,13 +55,14 @@ def tile_graph_conv_pb_t_kernel(tc, x0, x1, x2, laplacian, weight, bias, out):
         x2n = const.tile([P, 8, C * B], BF16)
         x2_words = x2n[:].bitcast(F32)
 
-        def load_x2(q):
-            nc.sync.dma_start(out=x2n[:, 2 * q:2 * q + 2, :],
-                              in_=x2[VB * q:VB * (q + 1), :].rearrange("(p e) n -> p e n", e=2))
-
         l_tiles = {}
         x1_tiles = {}
         x0_tiles = {}
+
+        def load_x2(q, h):
+            ns = slice(1024 * h, 1024 * (h + 1))
+            nc.sync.dma_start(out=x2n[:, 2 * q:2 * q + 2, ns],
+                              in_=x2[VB * q:VB * (q + 1), ns].rearrange("(p e) n -> p e n", e=2))
 
         def load_l(q):
             l_nat = chunk.tile([P, 2, V], BF16)
@@ -67,21 +74,27 @@ def tile_graph_conv_pb_t_kernel(tc, x0, x1, x2, laplacian, weight, bias, out):
             nc.sync.dma_start(out=x1c[:], in_=x1[VB * q:VB * (q + 1), :].rearrange("(t p) n -> p t n", p=P))
             x1_tiles[q] = x1c
 
-        def load_x0(q, bh):
+        def load_x0(i):
+            q, r = divmod(i, UPB)
             x0n = x0_pool.tile([P, UB, VB], BF16)
             nc.sync.dma_start(out=x0n[:],
-                              in_=x0[UB * bh:UB * (bh + 1), :, VB * q:VB * (q + 1)].rearrange("b c v -> c b v"))
-            x0_tiles[(q, bh)] = x0n
+                              in_=x0[UB * r:UB * (r + 1), :, VB * q:VB * (q + 1)].rearrange("b c v -> c b v"))
+            x0_tiles[i] = x0n
 
-        for q in range(4):
-            load_x2(q)
+        for g in range(2):
+            for h in range(2):
+                load_x2(2 * g, h)
+                load_x2(2 * g + 1, h)
         load_l(0)
         load_x1(0)
-        load_x0(0, 0)
-        load_x0(0, 1)
+        load_x0(0)
+        load_x0(1)
+        load_x0(2)
         load_l(1)
         load_x1(1)
-        load_x0(1, 0)
+        load_x0(3)
+        load_x0(4)
+        load_x0(5)
 
         w_words = w_nat[:].bitcast(F32)
         w_ps = ps_t.tile([P, 2, P], F32, tag="tp")
@@ -103,134 +116,217 @@ def tile_graph_conv_pb_t_kernel(tc, x0, x1, x2, laplacian, weight, bias, out):
         lt_codes = const.tile([P, 2, V], U32, align_bytes=64)
         lt_sc = const.tile([P, 2, V], U8, align_bytes=64)
 
-        def prep_x2(g):
-            x2g = big.tile([P, B, C, 4], BF16, tag="big", align_bytes=64)
-            src = x2n[:, 4 * g:4 * g + 4, :].rearrange("p j (c b) -> p b c j", b=B)
-            for hq in range(2):
-                b0 = 8 * hq
-                nc.vector.tensor_copy(out=x2g[:, b0:b0 + 4], in_=src[:, b0:b0 + 4])
-                nc.scalar.copy(out=x2g[:, b0 + 6:b0 + 8], in_=src[:, b0 + 6:b0 + 8])
-                nc.vector.tensor_copy(out=x2g[:, b0 + 4:b0 + 6], in_=src[:, b0 + 4:b0 + 6])
-                cs = slice(hq * 1024, (hq + 1) * 1024)
-                nc.vector.quantize_mx(out=x2_codes[:, g, cs].bitcast(FP8X4), scales=x2_sc[:, g, cs],
-                                      in_=x2g[:, b0:b0 + 8].rearrange("p b c j -> p (b c j)"))
+        x2g_tiles = {}
 
-        def prep_l(q):
+        def regroup_x2(g, h):
+            if h == 0:
+                x2g = x2g_pool.tile([P, B, C, 4], BF16, align_bytes=64)
+                x2g_tiles[g] = x2g
+            dst = x2g_tiles[g][:, :, 64 * h:64 * (h + 1), :]
+            src = x2n[:, 4 * g:4 * g + 4, 1024 * h:1024 * (h + 1)].rearrange("p j (c b) -> p b c j", b=B)
+            nc.vector.tensor_copy(out=dst[:, 0:V_B], in_=src[:, 0:V_B])
+            nc.scalar.copy(out=dst[:, V_B:B], in_=src[:, V_B:B])
+
+        def quant_x2(g, hq):
+            cs = slice(hq * 1024, (hq + 1) * 1024)
+            nc.vector.quantize_mx(out=x2_codes[:, g, cs].bitcast(FP8X4), scales=x2_sc[:, g, cs],
+                                  in_=x2g_tiles[g][:, 8 * hq:8 * hq + 8].rearrange("p b c j -> p (b c j)"))
+
+        tl_tiles = {}
+        ltg_tiles = {}
+
+        def t_l(q, g):
             l_words = l_tiles[q][:].bitcast(F32)
-            ltg = chunk.tile([P, 2, VB, 4], BF16, align_bytes=64)
-            ltg_words = ltg[:].bitcast(F32)
+            tp = ps_2.tile([P, 2, VB], F32, tag="m2")
+            tl_tiles[(q, g)] = tp
+            for s in range(2):
+                for tt in range(2):
+                    nc.tensor.transpose(tp[:, s, tt * P:(tt + 1) * P],
+                                        l_words[:, tt, 256 * g + 128 * s:256 * g + 128 * (s + 1)], ident[:])
+
+        def c_l(q, g):
+            if g == 0:
+                ltg = chunk.tile([P, 2, VB, 4], BF16, align_bytes=64)
+                ltg_tiles[q] = ltg
+            ltg_words = ltg_tiles[q][:].bitcast(F32)
+            nc.scalar.copy(out=ltg_words[:, g, :, :], in_=tl_tiles[(q, g)][:].rearrange("p s v -> p v s"))
+
+        def q_l(q):
             vs = slice(q * VB, (q + 1) * VB)
-            for g in range(2):
-                tp = ps_t.tile([P, 2, VB], F32, tag="tp")
-                for h in range(2):
-                    for tt in range(2):
-                        nc.tensor.transpose(tp[:, h, tt * P:(tt + 1) * P],
-                                            l_words[:, tt, 256 * g + 128 * h:256 * g + 128 * (h + 1)], ident[:])
-                nc.scalar.copy(out=ltg_words[:, g, :, :], in_=tp[:].rearrange("p h v -> p v h"))
             for g in range(2):
                 nc.vector.quantize_mx(out=lt_codes[:, g, vs].bitcast(FP8X4), scales=lt_sc[:, g, vs],
-                                      in_=ltg[:, g, :, :].rearrange("p v t -> p (v t)"))
+                                      in_=ltg_tiles[q][:, g, :, :].rearrange("p v t -> p (v t)"))
 
         planes = {}
+        tp2 = {}
+        tp1 = {}
+        m1s = {}
+        m2s = {}
         grouped = {}
+        codes = {}
 
-        def stage_a(q, bh):
-            xp = big.tile([P, K, COLS], BF16, tag="big", align_bytes=64)
-            planes[(q, bh)] = xp
-            xp_words = xp[:].bitcast(F32)
-            for lp in range(2):
-                tp = ps_t.tile([P, 2, 2, P], F32, tag="tp")
-                for l in range(2):
-                    bb = 4 * bh + 2 * lp + l
-                    for e in range(2):
-                        nc.tensor.transpose(tp[:, l, e, :], x2_words[:, 2 * q + e, bb:C * 8:8], ident[:])
-                nc.scalar.copy(out=xp_words[:, 2, lp * 512:(lp + 1) * 512].rearrange("p (l r e) -> p l r e", l=2, e=2),
-                               in_=tp[:].rearrange("p l e r -> p l r e"))
-            x1_words = x1_tiles[q][:].bitcast(F32)
-            for lp in range(2):
-                tp = ps_t.tile([P, 2, 2, P], F32, tag="tp")
-                for l in range(2):
-                    bb = 4 * bh + 2 * lp + l
-                    for tt in range(2):
-                        nc.tensor.transpose(tp[:, l, tt, :], x1_words[:, tt, bb:C * 8:8], ident[:])
-                nc.scalar.copy(out=xp_words[:, 1, lp * 512:(lp + 1) * 512],
-                               in_=tp[:].rearrange("p l t r -> p (l t r)"))
-            x0n = x0_tiles[(q, bh)]
-            nc.scalar.copy(out=xp[:, 0, :].rearrange("p (l v e) -> p l v e", l=4, e=2),
-                           in_=x0n[:].rearrange("p (l e) v -> p l v e", e=2))
-
-        def stage_b(q, bh):
-            xp = planes[(q, bh)]
-            vs = slice(q * VB, (q + 1) * VB)
-            for l in range(4):
-                m1 = ps_1.tile([P, 2, VB], F32, tag="m1")
+        def t_2(i):
+            q, r = divmod(i, UPB)
+            tp = ps_t.tile([P, 2, 2, P], F32, tag="tp")
+            tp2[i] = tp
+            for l in range(2):
                 for e in range(2):
-                    b = UB * bh + 2 * l + e
+                    nc.tensor.transpose(tp[:, l, e, :], x2_words[:, 2 * q + e, 2 * r + l:C * 8:8], ident[:])
+
+        def t_1(i):
+            q, r = divmod(i, UPB)
+            x1_words = x1_tiles[q][:].bitcast(F32)
+            tp = ps_t.tile([P, 2, 2, P], F32, tag="tp")
+            tp1[i] = tp
+            for l in range(2):
+                for tt in range(2):
+                    nc.tensor.transpose(tp[:, l, tt, :], x1_words[:, tt, 2 * r + l:C * 8:8], ident[:])
+
+        def c_2(i):
+            xp = big.tile([P, K, COLS], BF16, tag="big", align_bytes=64)
+            planes[i] = xp
+            nc.scalar.copy(out=xp[:].bitcast(F32)[:, 2, :].rearrange("p (l r e) -> p l r e", l=2, e=2),
+                           in_=tp2[i][:].rearrange("p l e r -> p l r e"))
+
+        def c_1(i):
+            nc.scalar.copy(out=planes[i][:].bitcast(F32)[:, 1, :], in_=tp1[i][:].rearrange("p l t r -> p (l t r)"))
+
+        def h_0(i):
+            nc.scalar.copy(out=planes[i][:, 0, :].rearrange("p (l v e) -> p l v e", l=2, e=2),
+                           in_=x0_tiles[i][:].rearrange("p (l e) v -> p l v e", e=2))
+
+        def m_1(i):
+            q, r = divmod(i, UPB)
+            vs = slice(q * VB, (q + 1) * VB)
+            for l in range(2):
+                m1 = ps_1.tile([P, 2, VB], F32, tag="m1")
+                m1s[(i, l)] = m1
+                for e in range(2):
+                    b = UB * r + 2 * l + e
                     bs = slice(b * C, (b + 1) * C)
                     for g in range(2):
                         nc.tensor.matmul_mx(out=m1[:, e, :],
                                             lhsT=x2_codes[:, g, bs].bitcast(FP8X4), lhsT_scale=x2_sc[:, g, bs],
                                             rhs=lt_codes[:, g, vs].bitcast(FP8X4), rhs_scale=lt_sc[:, g, vs],
                                             start=(g == 0), stop=(g == 1))
+
+        def e_3(i):
+            xp = planes[i]
+            for l in range(2):
                 ws = slice(l * 512, (l + 1) * 512)
-                nc.vector.scalar_tensor_tensor(out=xp[:, 3, ws], in0=m1[:].rearrange("p e v -> p v e"),
+                nc.vector.scalar_tensor_tensor(out=xp[:, 3, ws], in0=m1s[(i, l)][:].rearrange("p e v -> p v e"),
                                                scalar=2.0, in1=xp[:, 1, ws],
                                                op0=ALU.mult, op1=ALU.subtract)
 
-        def stage_c(q, bh):
-            xp = planes[(q, bh)]
+        def b_s(i):
             fg = big.tile([P, COLS, K], BF16, tag="big", align_bytes=64)
+            grouped[i] = fg
+            m = COLS - S_COLS
+            nc.scalar.copy(out=fg[:, m:COLS, :].rearrange("p (c i) t -> p c t i", i=4),
+                           in_=planes[i][:, :, m:COLS].rearrange("p t (c i) -> p c t i", i=4))
+
+        def b_v(i):
+            m = COLS - S_COLS
+            nc.vector.tensor_copy(out=grouped[i][:, 0:m, :].rearrange("p (c i) t -> p c t i", i=4),
+                                  in_=planes[i][:, :, 0:m].rearrange("p t (c i) -> p c t i", i=4))
+
+        def q_f(i):
             f_codes = f_pool.tile([P, COLS], U32, align_bytes=64)
             f_sc = f_pool.tile([P, COLS], U8, align_bytes=64)
-            grouped[(q, bh)] = (f_codes, f_sc)
-            for half in range(2):
-                a = half * 1024
-                m = a + 1024 - S_COLS
-                z = a + 1024
-                nc.vector.tensor_copy(out=fg[:, a:m, :].rearrange("p (c i) t -> p c t i", i=4),
-                                      in_=xp[:, :, a:m].rearrange("p t (c i) -> p c t i", i=4))
-                nc.scalar.copy(out=fg[:, m:z, :].rearrange("p (c i) t -> p c t i", i=4),
-                               in_=xp[:, :, m:z].rearrange("p t (c i) -> p c t i", i=4))
-            for half in range(2):
-                cs = slice(half * 1024, (half + 1) * 1024)
-                nc.vector.quantize_mx(out=f_codes[:, cs].bitcast(FP8X4), scales=f_sc[:, cs],
-                                      in_=fg[:, cs, :].rearrange("p w t -> p (w t)"))
+            codes[i] = (f_codes, f_sc)
+            nc.vector.quantize_mx(out=f_codes[:].bitcast(FP8X4), scales=f_sc[:],
+                                  in_=grouped[i][:].rearrange("p w t -> p (w t)"))
 
-        def stage_d(q, bh):
-            f_codes, f_sc = grouped[(q, bh)]
-            o_sb = o_pool.tile([P, UB, VB], F32)
-            for l in range(4):
+        def m_2(i):
+            f_codes, f_sc = codes[i]
+            for l in range(2):
                 cs = slice(l * 512, (l + 1) * 512)
                 m2 = ps_2.tile([P, 512], F32, tag="m2")
+                m2s[(i, l)] = m2
                 nc.tensor.matmul_mx(out=m2[:], lhsT=w_codes[:].bitcast(FP8X4), lhsT_scale=w_sc[:],
                                     rhs=f_codes[:, cs].bitcast(FP8X4), rhs_scale=f_sc[:, cs],
                                     start=True, stop=True)
-                nc.scalar.activation(out=o_sb[:, 2 * l:2 * l + 2, :],
-                                     in_=m2[:].rearrange("p (v e) -> p e v", e=2),
-                                     func=ACT.Identity, bias=bias_f[:, 0:1], scale=1.0)
-            nc.scalar.dma_start(out=out[UB * bh:UB * (bh + 1), :, VB * q:VB * (q + 1)].rearrange("b o v -> o b v"),
-                                in_=o_sb[:])
 
-        units = [(q, bh) for q in range(NVB) for bh in range(2)]
+        def f_o(i):
+            q, r = divmod(i, UPB)
+            o_sb = o_pool.tile([P, UB, VB], F32)
+            dst = out[UB * r:UB * (r + 1), :, VB * q:VB * (q + 1)].rearrange("b o v -> o b v")
+            for l in range(2):
+                src = m2s[(i, l)][:].rearrange("p (v e) -> p e v", e=2)
+                if i == NU - 1 and l == 1:
+                    nc.vector.tensor_scalar(out=o_sb[:, 2 * l:2 * l + 2, :], in0=src, scalar1=bias_f[:, 0:1],
+                                            scalar2=None, op0=ALU.add)
+                else:
+                    nc.scalar.activation(out=o_sb[:, 2 * l:2 * l + 2, :], in_=src,
+                                         func=ACT.Identity, bias=bias_f[:, 0:1], scale=1.0)
+                if i == NU - 1:
+                    nc.sync.dma_start(out=dst[:, 2 * l:2 * l + 2, :], in_=o_sb[:, 2 * l:2 * l + 2, :])
+            if i < NU - 1:
+                nc.sync.dma_start(out=dst, in_=o_sb[:])
 
-        prep_x2(0)
-        prep_l(0)
-        stage_a(0, 0)
-        prep_x2(1)
-        stage_a(0, 1)
-        for i in range(len(units)):
-            q, bh = units[i]
-            stage_b(q, bh)
-            if i + 2 < len(units):
-                q2, bh2 = units[i + 2]
-                if bh2 == 0:
-                    prep_l(q2)
-                    if q2 + 1 < NVB:
-                        load_l(q2 + 1)
-                        load_x1(q2 + 1)
-                stage_a(q2, bh2)
-                if i + 3 < len(units) and i + 3 >= 3:
-                    q3, bh3 = units[i + 3]
-                    load_x0(q3, bh3)
-            stage_c(q, bh)
-            stage_d(q, bh)
+        done = set()
+
+        def emit(fn, i):
+            if 0 <= i < NU and (fn, i) not in done:
+                done.add((fn, i))
+                fn(i)
+
+        regroup_x2(0, 0)
+        emit(t_2, 0)
+        emit(t_2, 1)
+        emit(c_2, 0)
+        emit(t_2, 2)
+        regroup_x2(0, 1)
+        emit(c_2, 1)
+        emit(c_2, 2)
+        quant_x2(0, 0)
+        regroup_x2(1, 0)
+        quant_x2(0, 1)
+        regroup_x2(1, 1)
+        t_l(0, 0)
+        t_l(0, 1)
+        c_l(0, 0)
+        c_l(0, 1)
+        quant_x2(1, 0)
+        q_l(0)
+        quant_x2(1, 1)
+        emit(t_1, 0)
+        emit(t_1, 1)
+        emit(c_1, 0)
+        emit(t_1, 2)
+        emit(m_1, 0)
+        emit(m_1, 1)
+        emit(c_1, 1)
+        emit(h_0, 0)
+        emit(e_3, 0)
+        emit(c_1, 2)
+        emit(h_0, 1)
+        emit(h_0, 2)
+
+        for i in range(NU + 1):
+            nq = i // UPB + 1
+            if i + X0_AHEAD < NU:
+                load_x0(i + X0_AHEAD)
+            if i == 1:
+                load_l(2)
+                load_x1(2)
+            if i == 5:
+                load_l(3)
+                load_x1(3)
+            emit(b_s, i)
+            emit(b_v, i)
+            emit(m_2, i - 1)
+            emit(m_1, i + 2)
+            emit(c_2, i + 2)
+            emit(c_1, i + 2)
+            emit(f_o, i - 1)
+            emit(e_3, i + 1)
+            emit(h_0, i + 2)
+            emit(t_2, i + 3)
+            emit(t_1, i + 3)
+            if i % UPB < 2 and nq < NVB:
+                t_l(nq, i % UPB)
+                c_l(nq, i % UPB)
+            emit(q_f, i)
+            if i % UPB == 1 and nq < NVB:
+                q_l(nq)

@@ -21,7 +21,7 @@ NU = NVB * UPB
 COLS = UB * VB
 FLOPS = 2 * V * V * C * B + 2 * B * V * C * K * OUT
 
-S_COLS = 192
+S_COLS = 352
 V_B = 10
 X0_AHEAD = 6
 
@@ -192,8 +192,10 @@ def tile_graph_conv_pb_t_kernel(tc, x0, x1, x2, laplacian, weight, bias, out):
             nc.scalar.copy(out=planes[i][:].bitcast(F32)[:, 1, :], in_=tp1[i][:].rearrange("p l t r -> p (l t r)"))
 
         def h_0(i):
-            nc.scalar.copy(out=planes[i][:, 0, :].rearrange("p (l v e) -> p l v e", l=2, e=2),
-                           in_=x0_tiles[i][:].rearrange("p (l e) v -> p l v e", e=2))
+            for l in range(2):
+                nc.gpsimd.tensor_scalar(out=planes[i][:, 0, l * 512:(l + 1) * 512].rearrange("p (v e) -> p v e", e=2),
+                                        in0=x0_tiles[i][:, 2 * l:2 * l + 2, :].rearrange("p e v -> p v e"),
+                                        scalar1=1.0, scalar2=0.0, op0=ALU.mult, op1=ALU.add)
 
         def m_1(i):
             q, r = divmod(i, UPB)

@@ -22,18 +22,16 @@ COLS = UB * VB
 FLOPS = 2 * V * V * C * B + 2 * B * V * C * K * OUT
 
 S_COLS = 352
-V_B = 10
-X0_AHEAD = 6
+RUN = 4
+X0_AHEAD = 5
 
 
 def tile_graph_conv_pb_t_kernel(tc, x0, x1, x2, laplacian, weight, bias, out):
     nc = tc.nc
     with ExitStack() as ctx:
         const = ctx.enter_context(tc.tile_pool(name="const", bufs=1))
-        x2g_pool = ctx.enter_context(tc.tile_pool(name="x2gp", bufs=2))
-        big = ctx.enter_context(tc.tile_pool(name="big", bufs=7))
+        big = ctx.enter_context(tc.tile_pool(name="big", bufs=9))
         chunk = ctx.enter_context(tc.tile_pool(name="chunk", bufs=2))
-        x0_pool = ctx.enter_context(tc.tile_pool(name="x0p", bufs=X0_AHEAD))
         f_pool = ctx.enter_context(tc.tile_pool(name="fp", bufs=3))
         o_pool = ctx.enter_context(tc.tile_pool(name="op", bufs=4))
         ps_t = ctx.enter_context(tc.psum_pool(name="pst", bufs=2))
@@ -46,6 +44,10 @@ def tile_graph_conv_pb_t_kernel(tc, x0, x1, x2, laplacian, weight, bias, out):
         ident_bf = const.tile([P, P], BF16)
         make_identity(nc, ident_bf[:])
 
+        warm = const.tile([P, 2], F32)
+        nc.vector.memset(warm[:], 0.0)
+        nc.scalar.activation(out=warm[:, 0:1], in_=warm[:, 1:2], func=ACT.Identity, scale=1.0)
+
         w_nat = const.tile([P, C * K], BF16)
         nc.scalar.dma_start(out=w_nat[:], in_=weight)
         bias_rows = const.tile([P, P], BF16)
@@ -53,11 +55,11 @@ def tile_graph_conv_pb_t_kernel(tc, x0, x1, x2, laplacian, weight, bias, out):
         nc.scalar.dma_start(out=bias_rows[0:1, :], in_=bias.rearrange("(r o) -> r o", r=1))
 
         x2n = const.tile([P, 8, C * B], BF16)
-        x2_words = x2n[:].bitcast(F32)
 
         l_tiles = {}
         x1_tiles = {}
-        x0_tiles = {}
+        x2_tiles = {}
+        planes = {}
 
         def load_x2(q, h):
             ns = slice(1024 * h, 1024 * (h + 1))
@@ -74,42 +76,53 @@ def tile_graph_conv_pb_t_kernel(tc, x0, x1, x2, laplacian, weight, bias, out):
             nc.sync.dma_start(out=x1c[:], in_=x1[VB * q:VB * (q + 1), :].rearrange("(t p) n -> p t n", p=P))
             x1_tiles[q] = x1c
 
+        def load_x2c(q):
+            x2c = chunk.tile([P, 2, C * B], BF16)
+            nc.sync.dma_start(out=x2c[:], in_=x2[VB * q:VB * (q + 1), :].rearrange("(t p) n -> p t n", p=P))
+            x2_tiles[q] = x2c
+
         def load_x0(i):
             q, r = divmod(i, UPB)
-            x0n = x0_pool.tile([P, UB, VB], BF16)
-            nc.sync.dma_start(out=x0n[:],
+            xp = big.tile([P, K, COLS], BF16, tag="big", align_bytes=64)
+            planes[i] = xp
+            nc.sync.dma_start(out=xp[:, 0, :].rearrange("p (b v) -> p b v", b=UB),
                               in_=x0[UB * r:UB * (r + 1), :, VB * q:VB * (q + 1)].rearrange("b c v -> c b v"))
-            x0_tiles[i] = x0n
 
         for g in range(2):
             for h in range(2):
                 load_x2(2 * g, h)
                 load_x2(2 * g + 1, h)
-        load_l(0)
+            if g == 0:
+                load_l(0)
         load_x1(0)
         load_x0(0)
+        load_x2c(0)
         load_x0(1)
         load_x0(2)
         load_l(1)
         load_x1(1)
+        load_x2c(1)
         load_x0(3)
         load_x0(4)
-        load_x0(5)
 
         w_words = w_nat[:].bitcast(F32)
-        w_ps = ps_t.tile([P, 2, P], F32, tag="tp")
-        for h in range(2):
-            nc.tensor.transpose(w_ps[:, h, :], w_words[:, h:2 * C:2], ident[:])
-        wg = const.tile([P, OUT, 4], BF16, align_bytes=64)
-        nc.scalar.copy(out=wg[:].bitcast(F32), in_=w_ps[:].rearrange("p h o -> p o h"))
         w_codes = const.tile([P, OUT], U32, align_bytes=64)
         w_sc = const.tile([P, OUT], U8, align_bytes=64)
-        nc.vector.quantize_mx(out=w_codes[:].bitcast(FP8X4), scales=w_sc[:],
-                              in_=wg[:].rearrange("p o t -> p (o t)"))
-        b_ps = ps_t.tile([P, P], BF16, tag="tp")
-        nc.tensor.transpose(b_ps[:], bias_rows[:], ident_bf[:])
         bias_f = const.tile([P, 1], F32)
-        nc.vector.tensor_copy(out=bias_f[:], in_=b_ps[:, 0:1])
+
+        def prepare_weight():
+            w_ps = ps_t.tile([P, 2, P], F32, tag="tp")
+            for h in range(2):
+                nc.tensor.transpose(w_ps[:, h, :], w_words[:, h:2 * C:2], ident[:])
+            wg = const.tile([P, OUT, 4], BF16, align_bytes=64)
+            nc.scalar.copy(out=wg[:].bitcast(F32), in_=w_ps[:].rearrange("p h o -> p o h"))
+            nc.vector.quantize_mx(out=w_codes[:].bitcast(FP8X4), scales=w_sc[:],
+                                  in_=wg[:].rearrange("p o t -> p (o t)"))
+
+        def prepare_bias():
+            b_ps = ps_t.tile([P, P], BF16, tag="tp")
+            nc.tensor.transpose(b_ps[:], bias_rows[:], ident_bf[:])
+            nc.vector.tensor_copy(out=bias_f[:], in_=b_ps[:, 0:1])
 
         x2_codes = const.tile([P, 2, B * C], U32, align_bytes=64)
         x2_sc = const.tile([P, 2, B * C], U8, align_bytes=64)
@@ -119,18 +132,24 @@ def tile_graph_conv_pb_t_kernel(tc, x0, x1, x2, laplacian, weight, bias, out):
         x2g_tiles = {}
 
         def regroup_x2(g, h):
-            if h == 0:
-                x2g = x2g_pool.tile([P, B, C, 4], BF16, align_bytes=64)
-                x2g_tiles[g] = x2g
-            dst = x2g_tiles[g][:, :, 64 * h:64 * (h + 1), :]
-            src = x2n[:, 4 * g:4 * g + 4, 1024 * h:1024 * (h + 1)].rearrange("p j (c b) -> p b c j", b=B)
-            nc.vector.tensor_copy(out=dst[:, 0:V_B], in_=src[:, 0:V_B])
-            nc.scalar.copy(out=dst[:, V_B:B], in_=src[:, V_B:B])
+            src = x2n[:, 4 * g:4 * g + 4, 1024 * h:1024 * (h + 1)].rearrange("p j (c b) -> p c j b", b=B)
+            for hq in range(2):
+                if h == 0:
+                    x2g = big.tile([P, B // 2, C, 4], BF16, tag="big", align_bytes=64)
+                    x2g_tiles[(g, hq)] = x2g
+                dst = x2g_tiles[(g, hq)][:, :, 64 * h:64 * (h + 1), :].rearrange("p b c j -> p c j b")
+                for n in range(2):
+                    bs = slice(8 * hq + RUN * n, 8 * hq + RUN * (n + 1))
+                    ds = slice(RUN * n, RUN * (n + 1))
+                    if hq == 0:
+                        nc.vector.tensor_copy(out=dst[:, :, :, ds], in_=src[:, :, :, bs])
+                    else:
+                        nc.scalar.copy(out=dst[:, :, :, ds], in_=src[:, :, :, bs])
 
         def quant_x2(g, hq):
             cs = slice(hq * 1024, (hq + 1) * 1024)
             nc.vector.quantize_mx(out=x2_codes[:, g, cs].bitcast(FP8X4), scales=x2_sc[:, g, cs],
-                                  in_=x2g_tiles[g][:, 8 * hq:8 * hq + 8].rearrange("p b c j -> p (b c j)"))
+                                  in_=x2g_tiles[(g, hq)][:].rearrange("p b c j -> p (b c j)"))
 
         tl_tiles = {}
         ltg_tiles = {}
@@ -157,7 +176,6 @@ def tile_graph_conv_pb_t_kernel(tc, x0, x1, x2, laplacian, weight, bias, out):
                 nc.vector.quantize_mx(out=lt_codes[:, g, vs].bitcast(FP8X4), scales=lt_sc[:, g, vs],
                                       in_=ltg_tiles[q][:, g, :, :].rearrange("p v t -> p (v t)"))
 
-        planes = {}
         tp2 = {}
         tp1 = {}
         m1s = {}
@@ -165,37 +183,26 @@ def tile_graph_conv_pb_t_kernel(tc, x0, x1, x2, laplacian, weight, bias, out):
         grouped = {}
         codes = {}
 
+        def transposes(rows, r):
+            tp = ps_t.tile([P, UB, 2, P], BF16, tag="tp")
+            for e in range(UB):
+                for t in range(2):
+                    nc.tensor.transpose(tp[:, e, t, :], rows[:, t, UB * r + e:C * B:B], ident_bf[:])
+            return tp
+
         def t_2(i):
-            q, r = divmod(i, UPB)
-            tp = ps_t.tile([P, 2, 2, P], F32, tag="tp")
-            tp2[i] = tp
-            for l in range(2):
-                for e in range(2):
-                    nc.tensor.transpose(tp[:, l, e, :], x2_words[:, 2 * q + e, 2 * r + l:C * 8:8], ident[:])
+            tp2[i] = transposes(x2_tiles[i // UPB], i % UPB)
 
         def t_1(i):
-            q, r = divmod(i, UPB)
-            x1_words = x1_tiles[q][:].bitcast(F32)
-            tp = ps_t.tile([P, 2, 2, P], F32, tag="tp")
-            tp1[i] = tp
-            for l in range(2):
-                for tt in range(2):
-                    nc.tensor.transpose(tp[:, l, tt, :], x1_words[:, tt, 2 * r + l:C * 8:8], ident[:])
+            tp1[i] = transposes(x1_tiles[i // UPB], i % UPB)
 
         def c_2(i):
-            xp = big.tile([P, K, COLS], BF16, tag="big", align_bytes=64)
-            planes[i] = xp
-            nc.scalar.copy(out=xp[:].bitcast(F32)[:, 2, :].rearrange("p (l r e) -> p l r e", l=2, e=2),
-                           in_=tp2[i][:].rearrange("p l e r -> p l r e"))
+            nc.scalar.copy(out=planes[i][:, 2, :].bitcast(F32),
+                           in_=tp2[i][:].rearrange("p e t r -> p (e t r)").bitcast(F32))
 
         def c_1(i):
-            nc.scalar.copy(out=planes[i][:].bitcast(F32)[:, 1, :], in_=tp1[i][:].rearrange("p l t r -> p (l t r)"))
-
-        def h_0(i):
-            for l in range(2):
-                nc.gpsimd.tensor_scalar(out=planes[i][:, 0, l * 512:(l + 1) * 512].rearrange("p (v e) -> p v e", e=2),
-                                        in0=x0_tiles[i][:, 2 * l:2 * l + 2, :].rearrange("p e v -> p v e"),
-                                        scalar1=1.0, scalar2=0.0, op0=ALU.mult, op1=ALU.add)
+            nc.scalar.copy(out=planes[i][:, 1, :].bitcast(F32),
+                           in_=tp1[i][:].rearrange("p e t r -> p (e t r)").bitcast(F32))
 
         def m_1(i):
             q, r = divmod(i, UPB)
@@ -216,7 +223,7 @@ def tile_graph_conv_pb_t_kernel(tc, x0, x1, x2, laplacian, weight, bias, out):
             xp = planes[i]
             for l in range(2):
                 ws = slice(l * 512, (l + 1) * 512)
-                nc.vector.scalar_tensor_tensor(out=xp[:, 3, ws], in0=m1s[(i, l)][:].rearrange("p e v -> p v e"),
+                nc.vector.scalar_tensor_tensor(out=xp[:, 3, ws], in0=m1s[(i, l)][:].rearrange("p e v -> p (e v)"),
                                                scalar=2.0, in1=xp[:, 1, ws],
                                                op0=ALU.mult, op1=ALU.subtract)
 
@@ -254,7 +261,7 @@ def tile_graph_conv_pb_t_kernel(tc, x0, x1, x2, laplacian, weight, bias, out):
             o_sb = o_pool.tile([P, UB, VB], F32)
             dst = out[UB * r:UB * (r + 1), :, VB * q:VB * (q + 1)].rearrange("b o v -> o b v")
             for l in range(2):
-                src = m2s[(i, l)][:].rearrange("p (v e) -> p e v", e=2)
+                src = m2s[(i, l)][:].rearrange("p (e v) -> p e v", e=2)
                 if i == NU - 1 and l == 1:
                     nc.vector.tensor_scalar(out=o_sb[:, 2 * l:2 * l + 2, :], in0=src, scalar1=bias_f[:, 0:1],
                                             scalar2=None, op0=ALU.add)
@@ -274,36 +281,33 @@ def tile_graph_conv_pb_t_kernel(tc, x0, x1, x2, laplacian, weight, bias, out):
                 fn(i)
 
         regroup_x2(0, 0)
-        emit(t_2, 0)
-        emit(t_2, 1)
-        emit(c_2, 0)
-        emit(t_2, 2)
         regroup_x2(0, 1)
-        emit(c_2, 1)
-        emit(c_2, 2)
         quant_x2(0, 0)
-        regroup_x2(1, 0)
-        quant_x2(0, 1)
-        regroup_x2(1, 1)
         t_l(0, 0)
         t_l(0, 1)
         c_l(0, 0)
         c_l(0, 1)
-        quant_x2(1, 0)
+        regroup_x2(1, 0)
         q_l(0)
-        quant_x2(1, 1)
+        regroup_x2(1, 1)
+        quant_x2(1, 0)
         emit(t_1, 0)
-        emit(t_1, 1)
+        emit(t_2, 0)
         emit(c_1, 0)
-        emit(t_1, 2)
+        emit(c_2, 0)
         emit(m_1, 0)
+        quant_x2(0, 1)
+        emit(t_1, 1)
+        emit(t_2, 1)
+        emit(e_3, 0)
+        quant_x2(1, 1)
         emit(m_1, 1)
         emit(c_1, 1)
-        emit(h_0, 0)
-        emit(e_3, 0)
-        emit(c_1, 2)
-        emit(h_0, 1)
-        emit(h_0, 2)
+        emit(c_2, 1)
+        prepare_weight()
+        prepare_bias()
+        emit(t_2, 2)
+        emit(t_1, 2)
 
         for i in range(NU + 1):
             nq = i // UPB + 1
@@ -312,9 +316,11 @@ def tile_graph_conv_pb_t_kernel(tc, x0, x1, x2, laplacian, weight, bias, out):
             if i == 1:
                 load_l(2)
                 load_x1(2)
+                load_x2c(2)
             if i == 5:
                 load_l(3)
                 load_x1(3)
+                load_x2c(3)
             emit(b_s, i)
             emit(b_v, i)
             emit(m_2, i - 1)
@@ -323,7 +329,6 @@ def tile_graph_conv_pb_t_kernel(tc, x0, x1, x2, laplacian, weight, bias, out):
             emit(c_1, i + 2)
             emit(f_o, i - 1)
             emit(e_3, i + 1)
-            emit(h_0, i + 2)
             emit(t_2, i + 3)
             emit(t_1, i + 3)
             if i % UPB < 2 and nq < NVB:

@@ -21,7 +21,7 @@ NU = NVB * UPB
 COLS = UB * VB
 FLOPS = 2 * V * V * C * B + 2 * B * V * C * K * OUT
 
-S_COLS = 352
+S_COLS = 448
 RUN = 4
 X0_AHEAD = 5
 
@@ -30,7 +30,10 @@ def tile_graph_conv_pb_t_kernel(tc, x0, x1, x2, laplacian, weight, bias, out):
     nc = tc.nc
     with ExitStack() as ctx:
         const = ctx.enter_context(tc.tile_pool(name="const", bufs=1))
-        big = ctx.enter_context(tc.tile_pool(name="big", bufs=9))
+        rows_pool = ctx.enter_context(tc.tile_pool(name="rows", bufs=2))
+        planes_pool = ctx.enter_context(tc.tile_pool(name="planes", bufs=X0_AHEAD + 1))
+        x1g_pool = ctx.enter_context(tc.tile_pool(name="x1gp", bufs=3))
+        grouped_pool = ctx.enter_context(tc.tile_pool(name="groupedp", bufs=2))
         chunk = ctx.enter_context(tc.tile_pool(name="chunk", bufs=2))
         f_pool = ctx.enter_context(tc.tile_pool(name="fp", bufs=3))
         o_pool = ctx.enter_context(tc.tile_pool(name="op", bufs=4))
@@ -54,16 +57,18 @@ def tile_graph_conv_pb_t_kernel(tc, x0, x1, x2, laplacian, weight, bias, out):
         nc.vector.memset(bias_rows[:], 0.0)
         nc.scalar.dma_start(out=bias_rows[0:1, :], in_=bias.rearrange("(r o) -> r o", r=1))
 
-        x2n = const.tile([P, 8, C * B], BF16)
-
         l_tiles = {}
         x1_tiles = {}
         x2_tiles = {}
         planes = {}
 
         def load_x2(q, h):
+            g, s = divmod(q, 2)
+            if s == 0 and h == 0:
+                x2n = rows_pool.tile([P, 4, C * B], BF16)
+                x2_tiles[g] = x2n
             ns = slice(1024 * h, 1024 * (h + 1))
-            nc.sync.dma_start(out=x2n[:, 2 * q:2 * q + 2, ns],
+            nc.sync.dma_start(out=x2_tiles[g][:, 2 * s:2 * s + 2, ns],
                               in_=x2[VB * q:VB * (q + 1), ns].rearrange("(p e) n -> p e n", e=2))
 
         def load_l(q):
@@ -73,17 +78,12 @@ def tile_graph_conv_pb_t_kernel(tc, x0, x1, x2, laplacian, weight, bias, out):
 
         def load_x1(q):
             x1c = chunk.tile([P, 2, C * B], BF16)
-            nc.sync.dma_start(out=x1c[:], in_=x1[VB * q:VB * (q + 1), :].rearrange("(t p) n -> p t n", p=P))
+            nc.sync.dma_start(out=x1c[:], in_=x1[VB * q:VB * (q + 1), :].rearrange("(p e) n -> p e n", e=2))
             x1_tiles[q] = x1c
-
-        def load_x2c(q):
-            x2c = chunk.tile([P, 2, C * B], BF16)
-            nc.sync.dma_start(out=x2c[:], in_=x2[VB * q:VB * (q + 1), :].rearrange("(t p) n -> p t n", p=P))
-            x2_tiles[q] = x2c
 
         def load_x0(i):
             q, r = divmod(i, UPB)
-            xp = big.tile([P, K, COLS], BF16, tag="big", align_bytes=64)
+            xp = planes_pool.tile([P, K, COLS], BF16, align_bytes=64)
             planes[i] = xp
             nc.sync.dma_start(out=xp[:, 0, :].rearrange("p (b v) -> p b v", b=UB),
                               in_=x0[UB * r:UB * (r + 1), :, VB * q:VB * (q + 1)].rearrange("b c v -> c b v"))
@@ -96,12 +96,10 @@ def tile_graph_conv_pb_t_kernel(tc, x0, x1, x2, laplacian, weight, bias, out):
                 load_l(0)
         load_x1(0)
         load_x0(0)
-        load_x2c(0)
         load_x0(1)
         load_x0(2)
         load_l(1)
         load_x1(1)
-        load_x2c(1)
         load_x0(3)
         load_x0(4)
 
@@ -129,27 +127,24 @@ def tile_graph_conv_pb_t_kernel(tc, x0, x1, x2, laplacian, weight, bias, out):
         lt_codes = const.tile([P, 2, V], U32, align_bytes=64)
         lt_sc = const.tile([P, 2, V], U8, align_bytes=64)
 
-        x2g_tiles = {}
+        x2g = const.tile([P, 2, B, C, 4], BF16, align_bytes=64)
+        x2g_words = x2g[:].rearrange("p g b c j -> p (g b c j)").bitcast(F32).rearrange(
+            "p (g b c s) -> p g b c s", g=2, b=B, s=2)
 
         def regroup_x2(g, h):
-            src = x2n[:, 4 * g:4 * g + 4, 1024 * h:1024 * (h + 1)].rearrange("p j (c b) -> p c j b", b=B)
-            for hq in range(2):
-                if h == 0:
-                    x2g = big.tile([P, B // 2, C, 4], BF16, tag="big", align_bytes=64)
-                    x2g_tiles[(g, hq)] = x2g
-                dst = x2g_tiles[(g, hq)][:, :, 64 * h:64 * (h + 1), :].rearrange("p b c j -> p c j b")
-                for n in range(2):
-                    bs = slice(8 * hq + RUN * n, 8 * hq + RUN * (n + 1))
-                    ds = slice(RUN * n, RUN * (n + 1))
-                    if hq == 0:
-                        nc.vector.tensor_copy(out=dst[:, :, :, ds], in_=src[:, :, :, bs])
-                    else:
-                        nc.scalar.copy(out=dst[:, :, :, ds], in_=src[:, :, :, bs])
+            src = x2_tiles[g][:, :, 1024 * h:1024 * (h + 1)].rearrange("p j (c b) -> p c j b", b=B)
+            dst = x2g[:, g, :, 64 * h:64 * (h + 1), :].rearrange("p b c j -> p c j b")
+            for n in range(B // RUN):
+                bs = slice(RUN * n, RUN * (n + 1))
+                if n < 2:
+                    nc.vector.tensor_copy(out=dst[:, :, :, bs], in_=src[:, :, :, bs])
+                else:
+                    nc.scalar.copy(out=dst[:, :, :, bs], in_=src[:, :, :, bs])
 
         def quant_x2(g, hq):
             cs = slice(hq * 1024, (hq + 1) * 1024)
             nc.vector.quantize_mx(out=x2_codes[:, g, cs].bitcast(FP8X4), scales=x2_sc[:, g, cs],
-                                  in_=x2g_tiles[(g, hq)][:].rearrange("p b c j -> p (b c j)"))
+                                  in_=x2g[:, g, 8 * hq:8 * hq + 8].rearrange("p b c j -> p (b c j)"))
 
         tl_tiles = {}
         ltg_tiles = {}
@@ -176,6 +171,7 @@ def tile_graph_conv_pb_t_kernel(tc, x0, x1, x2, laplacian, weight, bias, out):
                 nc.vector.quantize_mx(out=lt_codes[:, g, vs].bitcast(FP8X4), scales=lt_sc[:, g, vs],
                                       in_=ltg_tiles[q][:, g, :, :].rearrange("p v t -> p (v t)"))
 
+        x1gs = {}
         tp2 = {}
         tp1 = {}
         m1s = {}
@@ -183,26 +179,33 @@ def tile_graph_conv_pb_t_kernel(tc, x0, x1, x2, laplacian, weight, bias, out):
         grouped = {}
         codes = {}
 
-        def transposes(rows, r):
-            tp = ps_t.tile([P, UB, 2, P], BF16, tag="tp")
-            for e in range(UB):
-                for t in range(2):
-                    nc.tensor.transpose(tp[:, e, t, :], rows[:, t, UB * r + e:C * B:B], ident_bf[:])
-            return tp
+        def g_1(i):
+            q, r = divmod(i, UPB)
+            x1g = x1g_pool.tile([P, UB, C, 2], BF16, align_bytes=64)
+            x1gs[i] = x1g
+            src = x1_tiles[q][:].rearrange("p j (c b) -> p c j b", b=B)
+            nc.vector.tensor_copy(out=x1g[:].rearrange("p e c j -> p c j e"), in_=src[:, :, :, UB * r:UB * (r + 1)])
 
         def t_2(i):
-            tp2[i] = transposes(x2_tiles[i // UPB], i % UPB)
+            q, r = divmod(i, UPB)
+            g, s = divmod(q, 2)
+            tp = ps_t.tile([P, UB, P], F32, tag="tp")
+            tp2[i] = tp
+            for e in range(UB):
+                nc.tensor.transpose(tp[:, e, :], x2g_words[:, g, UB * r + e, :, s], ident[:])
 
         def t_1(i):
-            tp1[i] = transposes(x1_tiles[i // UPB], i % UPB)
+            x1g_words = x1gs[i][:].rearrange("p e c j -> p (e c j)").bitcast(F32)
+            tp = ps_t.tile([P, UB, P], F32, tag="tp")
+            tp1[i] = tp
+            for e in range(UB):
+                nc.tensor.transpose(tp[:, e, :], x1g_words[:, C * e:C * (e + 1)], ident[:])
 
         def c_2(i):
-            nc.scalar.copy(out=planes[i][:, 2, :].bitcast(F32),
-                           in_=tp2[i][:].rearrange("p e t r -> p (e t r)").bitcast(F32))
+            nc.scalar.copy(out=planes[i][:, 2, :].bitcast(F32), in_=tp2[i][:].rearrange("p e r -> p (e r)"))
 
         def c_1(i):
-            nc.scalar.copy(out=planes[i][:, 1, :].bitcast(F32),
-                           in_=tp1[i][:].rearrange("p e t r -> p (e t r)").bitcast(F32))
+            nc.scalar.copy(out=planes[i][:, 1, :].bitcast(F32), in_=tp1[i][:].rearrange("p e r -> p (e r)"))
 
         def m_1(i):
             q, r = divmod(i, UPB)
@@ -228,7 +231,7 @@ def tile_graph_conv_pb_t_kernel(tc, x0, x1, x2, laplacian, weight, bias, out):
                                                op0=ALU.mult, op1=ALU.subtract)
 
         def b_s(i):
-            fg = big.tile([P, COLS, K], BF16, tag="big", align_bytes=64)
+            fg = grouped_pool.tile([P, COLS, K], BF16, align_bytes=64)
             grouped[i] = fg
             m = COLS - S_COLS
             nc.scalar.copy(out=fg[:, m:COLS, :].rearrange("p (c i) t -> p c t i", i=4),
@@ -287,27 +290,32 @@ def tile_graph_conv_pb_t_kernel(tc, x0, x1, x2, laplacian, weight, bias, out):
         t_l(0, 1)
         c_l(0, 0)
         c_l(0, 1)
+        emit(t_2, 0)
+        emit(t_2, 1)
         regroup_x2(1, 0)
         q_l(0)
         regroup_x2(1, 1)
-        quant_x2(1, 0)
-        emit(t_1, 0)
-        emit(t_2, 0)
-        emit(c_1, 0)
         emit(c_2, 0)
+        emit(t_2, 2)
+        quant_x2(1, 0)
+        emit(g_1, 0)
+        emit(t_1, 0)
+        emit(c_2, 1)
+        emit(c_1, 0)
         emit(m_1, 0)
+        emit(g_1, 1)
         quant_x2(0, 1)
         emit(t_1, 1)
-        emit(t_2, 1)
         emit(e_3, 0)
+        emit(g_1, 2)
         quant_x2(1, 1)
         emit(m_1, 1)
+        emit(c_2, 2)
         emit(c_1, 1)
-        emit(c_2, 1)
         prepare_weight()
-        prepare_bias()
-        emit(t_2, 2)
+        emit(g_1, 3)
         emit(t_1, 2)
+        prepare_bias()
 
         for i in range(NU + 1):
             nq = i // UPB + 1
@@ -316,11 +324,9 @@ def tile_graph_conv_pb_t_kernel(tc, x0, x1, x2, laplacian, weight, bias, out):
             if i == 1:
                 load_l(2)
                 load_x1(2)
-                load_x2c(2)
             if i == 5:
                 load_l(3)
                 load_x1(3)
-                load_x2c(3)
             emit(b_s, i)
             emit(b_v, i)
             emit(m_2, i - 1)
@@ -329,6 +335,7 @@ def tile_graph_conv_pb_t_kernel(tc, x0, x1, x2, laplacian, weight, bias, out):
             emit(c_1, i + 2)
             emit(f_o, i - 1)
             emit(e_3, i + 1)
+            emit(g_1, i + 4)
             emit(t_2, i + 3)
             emit(t_1, i + 3)
             if i % UPB < 2 and nq < NVB:

@@ -21,7 +21,7 @@ NU = NVB * UPB
 COLS = UB * VB
 FLOPS = 2 * V * V * C * B + 2 * B * V * C * K * OUT
 
-S_COLS = 448
+S_COLS = 368
 RUN = 4
 X0_AHEAD = 5
 

@@ -13,6 +13,7 @@ ACT = mybir.ActivationFunctionType
 
 P = 128
 B, C, V, K, OUT = 16, 128, 1024, 4, 128
+HC = C // 2
 VB = 256
 NVB = V // VB
 UB = 4
@@ -21,24 +22,22 @@ NU = NVB * UPB
 COLS = UB * VB
 FLOPS = 2 * V * V * C * B + 2 * B * V * C * K * OUT
 
-S_COLS = 368
-RUN = 4
-X0_AHEAD = 5
+LEAD = 3
+X0_AHEAD = 7
 
 
 def tile_graph_conv_pb_t_kernel(tc, x0, x1, x2, laplacian, weight, bias, out):
     nc = tc.nc
     with ExitStack() as ctx:
         const = ctx.enter_context(tc.tile_pool(name="const", bufs=1))
-        rows_pool = ctx.enter_context(tc.tile_pool(name="rows", bufs=2))
-        planes_pool = ctx.enter_context(tc.tile_pool(name="planes", bufs=X0_AHEAD + 1))
-        x1g_pool = ctx.enter_context(tc.tile_pool(name="x1gp", bufs=3))
-        grouped_pool = ctx.enter_context(tc.tile_pool(name="groupedp", bufs=2))
         chunk = ctx.enter_context(tc.tile_pool(name="chunk", bufs=2))
+        x0_pool = ctx.enter_context(tc.tile_pool(name="x0p", bufs=6))
+        feat_pool = ctx.enter_context(tc.tile_pool(name="featp", bufs=4))
+        grouped_pool = ctx.enter_context(tc.tile_pool(name="groupedp", bufs=2))
         f_pool = ctx.enter_context(tc.tile_pool(name="fp", bufs=3))
-        o_pool = ctx.enter_context(tc.tile_pool(name="op", bufs=4))
-        ps_t = ctx.enter_context(tc.psum_pool(name="pst", bufs=2))
-        ps_1 = ctx.enter_context(tc.psum_pool(name="ps1", bufs=4))
+        o_pool = ctx.enter_context(tc.tile_pool(name="op", bufs=3))
+        ps_t = ctx.enter_context(tc.psum_pool(name="pst", bufs=4))
+        ps_1 = ctx.enter_context(tc.psum_pool(name="ps1", bufs=2))
         ps_2 = ctx.enter_context(tc.psum_pool(name="ps2", bufs=2))
         ctx.enter_context(tc.manual_schedule())
 
@@ -46,6 +45,9 @@ def tile_graph_conv_pb_t_kernel(tc, x0, x1, x2, laplacian, weight, bias, out):
         make_identity(nc, ident[:])
         ident_bf = const.tile([P, P], BF16)
         make_identity(nc, ident_bf[:])
+        perm = const.tile([P, P], BF16)
+        nc.gpsimd.tensor_copy(out=perm[:].rearrange("p (l u) -> p l u", u=2),
+                              in_=ident_bf[:].rearrange("p (u l) -> p l u", u=2))
 
         warm = const.tile([P, 2], F32)
         nc.vector.memset(warm[:], 0.0)
@@ -57,23 +59,20 @@ def tile_graph_conv_pb_t_kernel(tc, x0, x1, x2, laplacian, weight, bias, out):
         nc.vector.memset(bias_rows[:], 0.0)
         nc.scalar.dma_start(out=bias_rows[0:1, :], in_=bias.rearrange("(r o) -> r o", r=1))
 
+        x2n = const.tile([P, 2, 2, 4, HC * B], BF16)
         l_tiles = {}
         x1_tiles = {}
-        x2_tiles = {}
-        planes = {}
+        x0_tiles = {}
 
         def load_x2(q, h):
             g, s = divmod(q, 2)
-            if s == 0 and h == 0:
-                x2n = rows_pool.tile([P, 4, C * B], BF16)
-                x2_tiles[g] = x2n
             ns = slice(1024 * h, 1024 * (h + 1))
-            nc.sync.dma_start(out=x2_tiles[g][:, 2 * s:2 * s + 2, ns],
+            nc.sync.dma_start(out=x2n[:, g, h, 2 * s:2 * s + 2, :],
                               in_=x2[VB * q:VB * (q + 1), ns].rearrange("(p e) n -> p e n", e=2))
 
         def load_l(q):
             l_nat = chunk.tile([P, 2, V], BF16)
-            nc.sync.dma_start(out=l_nat[:], in_=laplacian[VB * q:VB * (q + 1), :].rearrange("(t p) u -> p t u", p=P))
+            nc.sync.dma_start(out=l_nat[:], in_=laplacian[VB * q:VB * (q + 1), :].rearrange("(p e) u -> p e u", e=2))
             l_tiles[q] = l_nat
 
         def load_x1(q):
@@ -83,10 +82,10 @@ def tile_graph_conv_pb_t_kernel(tc, x0, x1, x2, laplacian, weight, bias, out):
 
         def load_x0(i):
             q, r = divmod(i, UPB)
-            xp = planes_pool.tile([P, K, COLS], BF16, align_bytes=64)
-            planes[i] = xp
-            nc.sync.dma_start(out=xp[:, 0, :].rearrange("p (b v) -> p b v", b=UB),
+            x0n = x0_pool.tile([P, UB, VB], BF16)
+            nc.sync.dma_start(out=x0n[:],
                               in_=x0[UB * r:UB * (r + 1), :, VB * q:VB * (q + 1)].rearrange("b c v -> c b v"))
+            x0_tiles[i] = x0n
 
         for g in range(2):
             for h in range(2):
@@ -95,23 +94,23 @@ def tile_graph_conv_pb_t_kernel(tc, x0, x1, x2, laplacian, weight, bias, out):
             if g == 0:
                 load_l(0)
         load_x1(0)
-        load_x0(0)
-        load_x0(1)
-        load_x0(2)
+        for i in range(4):
+            load_x0(i)
         load_l(1)
         load_x1(1)
-        load_x0(3)
-        load_x0(4)
 
-        w_words = w_nat[:].bitcast(F32)
         w_codes = const.tile([P, OUT], U32, align_bytes=64)
         w_sc = const.tile([P, OUT], U8, align_bytes=64)
         bias_f = const.tile([P, 1], F32)
 
         def prepare_weight():
+            w_p = const.tile([P, C * K], BF16)
+            nc.vector.tensor_copy(out=w_p[:].rearrange("p (k l u) -> p k l u", k=K, u=2),
+                                  in_=w_nat[:].rearrange("p (u l k) -> p k l u", u=2, k=K))
+            w_words = w_p[:].bitcast(F32)
             w_ps = ps_t.tile([P, 2, P], F32, tag="tp")
             for h in range(2):
-                nc.tensor.transpose(w_ps[:, h, :], w_words[:, h:2 * C:2], ident[:])
+                nc.tensor.transpose(w_ps[:, h, :], w_words[:, P * h:P * (h + 1)], ident[:])
             wg = const.tile([P, OUT, 4], BF16, align_bytes=64)
             nc.scalar.copy(out=wg[:].bitcast(F32), in_=w_ps[:].rearrange("p h o -> p o h"))
             nc.vector.quantize_mx(out=w_codes[:].bitcast(FP8X4), scales=w_sc[:],
@@ -128,14 +127,12 @@ def tile_graph_conv_pb_t_kernel(tc, x0, x1, x2, laplacian, weight, bias, out):
         lt_sc = const.tile([P, 2, V], U8, align_bytes=64)
 
         x2g = const.tile([P, 2, B, C, 4], BF16, align_bytes=64)
-        x2g_words = x2g[:].rearrange("p g b c j -> p (g b c j)").bitcast(F32).rearrange(
-            "p (g b c s) -> p g b c s", g=2, b=B, s=2)
 
-        def regroup_x2(g, h):
-            src = x2_tiles[g][:, :, 1024 * h:1024 * (h + 1)].rearrange("p j (c b) -> p c j b", b=B)
-            dst = x2g[:, g, :, 64 * h:64 * (h + 1), :].rearrange("p b c j -> p c j b")
-            for n in range(B // RUN):
-                bs = slice(RUN * n, RUN * (n + 1))
+        def regroup_x2(g):
+            src = x2n[:, g].rearrange("p u j (l b) -> p l (u j) b", b=B)
+            dst = x2g[:, g].rearrange("p b (l u) j -> p l (u j) b", u=2)
+            for n in range(UPB):
+                bs = slice(UB * n, UB * (n + 1))
                 if n < 2:
                     nc.vector.tensor_copy(out=dst[:, :, :, bs], in_=src[:, :, :, bs])
                 else:
@@ -151,12 +148,12 @@ def tile_graph_conv_pb_t_kernel(tc, x0, x1, x2, laplacian, weight, bias, out):
 
         def t_l(q, g):
             l_words = l_tiles[q][:].bitcast(F32)
-            tp = ps_2.tile([P, 2, VB], F32, tag="m2")
+            tp = ps_t.tile([P, 2, VB], F32, tag="tp")
             tl_tiles[(q, g)] = tp
             for s in range(2):
-                for tt in range(2):
-                    nc.tensor.transpose(tp[:, s, tt * P:(tt + 1) * P],
-                                        l_words[:, tt, 256 * g + 128 * s:256 * g + 128 * (s + 1)], ident[:])
+                for e in range(2):
+                    nc.tensor.transpose(tp[:, s, e * P:(e + 1) * P],
+                                        l_words[:, e, 256 * g + 128 * s:256 * g + 128 * (s + 1)], ident[:])
 
         def c_l(q, g):
             if g == 0:
@@ -171,76 +168,88 @@ def tile_graph_conv_pb_t_kernel(tc, x0, x1, x2, laplacian, weight, bias, out):
                 nc.vector.quantize_mx(out=lt_codes[:, g, vs].bitcast(FP8X4), scales=lt_sc[:, g, vs],
                                       in_=ltg_tiles[q][:, g, :, :].rearrange("p v t -> p (v t)"))
 
-        x1gs = {}
-        tp2 = {}
-        tp1 = {}
+        feats = {}
+        x0_ps = {}
+        f_ps = {}
         m1s = {}
         m2s = {}
         grouped = {}
+        fg_tiles = {}
         codes = {}
 
+        def feat_words(i):
+            return feats[i][:].rearrange("p e b k c -> p (e b k c)").bitcast(F32).rearrange(
+                "p (e b w) -> p e b w", e=2, b=UB)
+
+        def gather(i, k, rows):
+            r = i % UPB
+            for e in range(2):
+                nc.vector.tensor_copy(
+                    out=feats[i][:, e, :, k, :].rearrange("p b (l u) -> p l u b", u=2),
+                    in_=rows[:, :, e, :].rearrange("p u (l b) -> p l u b", b=B)[:, :, :, UB * r:UB * (r + 1)])
+
         def g_1(i):
-            q, r = divmod(i, UPB)
-            x1g = x1g_pool.tile([P, UB, C, 2], BF16, align_bytes=64)
-            x1gs[i] = x1g
-            src = x1_tiles[q][:].rearrange("p j (c b) -> p c j b", b=B)
-            nc.vector.tensor_copy(out=x1g[:].rearrange("p e c j -> p c j e"), in_=src[:, :, :, UB * r:UB * (r + 1)])
+            feat = feat_pool.tile([P, 2, UB, K, C], BF16, align_bytes=64)
+            feats[i] = feat
+            gather(i, 1, x1_tiles[i // UPB][:].rearrange("p e (u n) -> p u e n", u=2))
 
-        def t_2(i):
-            q, r = divmod(i, UPB)
-            g, s = divmod(q, 2)
-            tp = ps_t.tile([P, UB, P], F32, tag="tp")
-            tp2[i] = tp
-            for e in range(UB):
-                nc.tensor.transpose(tp[:, e, :], x2g_words[:, g, UB * r + e, :, s], ident[:])
+        def g_2(i):
+            g, s = divmod(i // UPB, 2)
+            gather(i, 2, x2n[:, g, :, 2 * s:2 * s + 2, :])
 
-        def t_1(i):
-            x1g_words = x1gs[i][:].rearrange("p e c j -> p (e c j)").bitcast(F32)
-            tp = ps_t.tile([P, UB, P], F32, tag="tp")
-            tp1[i] = tp
-            for e in range(UB):
-                nc.tensor.transpose(tp[:, e, :], x1g_words[:, C * e:C * (e + 1)], ident[:])
+        def t_0(i):
+            tp = ps_t.tile([P, 2, UB, C], BF16, tag="tp")
+            x0_ps[i] = tp
+            for e in range(2):
+                for b in range(UB):
+                    nc.tensor.transpose(tp[:, e, b, :], x0_tiles[i][:, b, e:VB:2], perm[:])
 
-        def c_2(i):
-            nc.scalar.copy(out=planes[i][:, 2, :].bitcast(F32), in_=tp2[i][:].rearrange("p e r -> p (e r)"))
-
-        def c_1(i):
-            nc.scalar.copy(out=planes[i][:, 1, :].bitcast(F32), in_=tp1[i][:].rearrange("p e r -> p (e r)"))
+        def c_0(i):
+            words = feat_words(i).rearrange("p e b (k l) -> p (e b) k l", k=K)
+            nc.scalar.copy(out=words[:, :, 0, :],
+                           in_=x0_ps[i][:].rearrange("p e b c -> p (e b c)").bitcast(F32).rearrange(
+                               "p (n l) -> p n l", l=HC))
 
         def m_1(i):
             q, r = divmod(i, UPB)
-            vs = slice(q * VB, (q + 1) * VB)
-            for l in range(2):
-                m1 = ps_1.tile([P, 2, VB], F32, tag="m1")
-                m1s[(i, l)] = m1
-                for e in range(2):
-                    b = UB * r + 2 * l + e
-                    bs = slice(b * C, (b + 1) * C)
-                    for g in range(2):
-                        nc.tensor.matmul_mx(out=m1[:, e, :],
-                                            lhsT=x2_codes[:, g, bs].bitcast(FP8X4), lhsT_scale=x2_sc[:, g, bs],
-                                            rhs=lt_codes[:, g, vs].bitcast(FP8X4), rhs_scale=lt_sc[:, g, vs],
-                                            start=(g == 0), stop=(g == 1))
+            ns = slice(UB * C * r, UB * C * (r + 1))
+            for e in range(2):
+                m1 = ps_1.tile([P, UB, C], F32, tag="m1")
+                m1s[(i, e)] = m1
+                vs = slice(VB * q + P * e, VB * q + P * (e + 1))
+                for g in range(2):
+                    nc.tensor.matmul_mx(out=m1[:].rearrange("p b c -> p (b c)"),
+                                        lhsT=lt_codes[:, g, vs].bitcast(FP8X4), lhsT_scale=lt_sc[:, g, vs],
+                                        rhs=x2_codes[:, g, ns].bitcast(FP8X4), rhs_scale=x2_sc[:, g, ns],
+                                        start=(g == 0), stop=(g == 1))
 
         def e_3(i):
-            xp = planes[i]
-            for l in range(2):
-                ws = slice(l * 512, (l + 1) * 512)
-                nc.vector.scalar_tensor_tensor(out=xp[:, 3, ws], in0=m1s[(i, l)][:].rearrange("p e v -> p (e v)"),
-                                               scalar=2.0, in1=xp[:, 1, ws],
-                                               op0=ALU.mult, op1=ALU.subtract)
+            for e in range(2):
+                nc.vector.scalar_tensor_tensor(out=feats[i][:, e, :, 3, :], in0=m1s[(i, e)][:], scalar=2.0,
+                                               in1=feats[i][:, e, :, 1, :], op0=ALU.mult, op1=ALU.subtract)
 
-        def b_s(i):
+        def t_f(i):
+            words = feat_words(i)
+            for b in range(UB):
+                tp = ps_t.tile([P, 2, 2, P], F32, tag="tp")
+                f_ps[(i, b)] = tp
+                for e in range(2):
+                    for h in range(2):
+                        nc.tensor.transpose(tp[:, e, h, :], words[:, e, b, P * h:P * (h + 1)], ident[:])
+
+        def a_f(i):
             fg = grouped_pool.tile([P, COLS, K], BF16, align_bytes=64)
             grouped[i] = fg
-            m = COLS - S_COLS
-            nc.scalar.copy(out=fg[:, m:COLS, :].rearrange("p (c i) t -> p c t i", i=4),
-                           in_=planes[i][:, :, m:COLS].rearrange("p t (c i) -> p c t i", i=4))
+            fg_words = fg[:].rearrange("p w t -> p (w t)").bitcast(F32).rearrange(
+                "p (b e n h) -> p b e n h", b=UB, e=2, h=2)
+            fg_tiles[i] = fg_words
 
-        def b_v(i):
-            m = COLS - S_COLS
-            nc.vector.tensor_copy(out=grouped[i][:, 0:m, :].rearrange("p (c i) t -> p c t i", i=4),
-                                  in_=planes[i][:, :, 0:m].rearrange("p t (c i) -> p c t i", i=4))
+        def c_f(i, b):
+            src = f_ps[(i, b)][:].rearrange("p e h n -> p e n h")
+            if b < UB - 1:
+                nc.scalar.copy(out=fg_tiles[i][:, b], in_=src)
+            else:
+                nc.vector.tensor_copy(out=fg_tiles[i][:, b], in_=src)
 
         def q_f(i):
             f_codes = f_pool.tile([P, COLS], U32, align_bytes=64)
@@ -264,83 +273,65 @@ def tile_graph_conv_pb_t_kernel(tc, x0, x1, x2, laplacian, weight, bias, out):
             o_sb = o_pool.tile([P, UB, VB], F32)
             dst = out[UB * r:UB * (r + 1), :, VB * q:VB * (q + 1)].rearrange("b o v -> o b v")
             for l in range(2):
-                src = m2s[(i, l)][:].rearrange("p (e v) -> p e v", e=2)
+                src = m2s[(i, l)][:].rearrange("p (b e n) -> p b n e", b=2, e=2)
+                osl = o_sb[:, 2 * l:2 * l + 2, :].rearrange("p b (n e) -> p b n e", e=2)
                 if i == NU - 1 and l == 1:
-                    nc.vector.tensor_scalar(out=o_sb[:, 2 * l:2 * l + 2, :], in0=src, scalar1=bias_f[:, 0:1],
-                                            scalar2=None, op0=ALU.add)
+                    nc.vector.tensor_scalar(out=osl, in0=src, scalar1=bias_f[:, 0:1], scalar2=None, op0=ALU.add)
                 else:
-                    nc.scalar.activation(out=o_sb[:, 2 * l:2 * l + 2, :], in_=src,
-                                         func=ACT.Identity, bias=bias_f[:, 0:1], scale=1.0)
+                    nc.scalar.activation(out=osl, in_=src, func=ACT.Identity, bias=bias_f[:, 0:1], scale=1.0)
                 if i == NU - 1:
                     nc.sync.dma_start(out=dst[:, 2 * l:2 * l + 2, :], in_=o_sb[:, 2 * l:2 * l + 2, :])
             if i < NU - 1:
                 nc.sync.dma_start(out=dst, in_=o_sb[:])
 
-        done = set()
+        def emit(fn, i, *args):
+            if 0 <= i < NU:
+                fn(i, *args)
 
-        def emit(fn, i):
-            if 0 <= i < NU and (fn, i) not in done:
-                done.add((fn, i))
-                fn(i)
-
-        regroup_x2(0, 0)
-        regroup_x2(0, 1)
+        regroup_x2(0)
         quant_x2(0, 0)
         t_l(0, 0)
         t_l(0, 1)
         c_l(0, 0)
         c_l(0, 1)
-        emit(t_2, 0)
-        emit(t_2, 1)
-        regroup_x2(1, 0)
         q_l(0)
-        regroup_x2(1, 1)
-        emit(c_2, 0)
-        emit(t_2, 2)
+        regroup_x2(1)
         quant_x2(1, 0)
-        emit(g_1, 0)
-        emit(t_1, 0)
-        emit(c_2, 1)
-        emit(c_1, 0)
-        emit(m_1, 0)
-        emit(g_1, 1)
         quant_x2(0, 1)
-        emit(t_1, 1)
-        emit(e_3, 0)
-        emit(g_1, 2)
-        quant_x2(1, 1)
-        emit(m_1, 1)
-        emit(c_2, 2)
-        emit(c_1, 1)
-        prepare_weight()
-        emit(g_1, 3)
-        emit(t_1, 2)
-        prepare_bias()
 
-        for i in range(NU + 1):
-            nq = i // UPB + 1
+        for i in range(-LEAD, NU + 1):
+            nq = (i + 6) // UPB
             if i + X0_AHEAD < NU:
                 load_x0(i + X0_AHEAD)
-            if i == 1:
+            if i == 0:
                 load_l(2)
+            if i == 1:
                 load_x1(2)
-            if i == 5:
+            if i == 4:
                 load_l(3)
+            if i == 5:
                 load_x1(3)
-            emit(b_s, i)
-            emit(b_v, i)
-            emit(m_2, i - 1)
-            emit(m_1, i + 2)
-            emit(c_2, i + 2)
-            emit(c_1, i + 2)
             emit(f_o, i - 1)
-            emit(e_3, i + 1)
-            emit(g_1, i + 4)
-            emit(t_2, i + 3)
-            emit(t_1, i + 3)
-            if i % UPB < 2 and nq < NVB:
-                t_l(nq, i % UPB)
-                c_l(nq, i % UPB)
+            emit(t_f, i + 1)
+            emit(e_3, i + 2)
+            emit(a_f, i + 1)
+            for b in range(UB - 1):
+                emit(c_f, i + 1, b)
             emit(q_f, i)
-            if i % UPB == 1 and nq < NVB:
+            emit(c_f, i + 1, UB - 1)
+            emit(g_1, i + 3)
+            emit(t_0, i + 3)
+            if (i + 6) % UPB < 2 and 1 <= nq < NVB:
+                t_l(nq, (i + 6) % UPB)
+                c_l(nq, (i + 6) % UPB)
+            emit(c_0, i + 3)
+            if (i + 6) % UPB == 2 and 1 <= nq < NVB:
                 q_l(nq)
+            if i == -3:
+                quant_x2(1, 1)
+            if i == -1:
+                prepare_weight()
+                prepare_bias()
+            emit(g_2, i + 3)
+            emit(m_1, i + 3)
+            emit(m_2, i)

@@ -22,8 +22,9 @@ NU = NVB * UPB
 COLS = UB * VB
 FLOPS = 2 * V * V * C * B + 2 * B * V * C * K * OUT
 
-LEAD = 3
-X0_AHEAD = 7
+X0_AHEAD = 6
+V_RUNS = 2
+V_FIRST = 1
 
 
 def tile_graph_conv_pb_t_kernel(tc, x0, x1, x2, laplacian, weight, bias, out):
@@ -87,23 +88,24 @@ def tile_graph_conv_pb_t_kernel(tc, x0, x1, x2, laplacian, weight, bias, out):
                               in_=x0[UB * r:UB * (r + 1), :, VB * q:VB * (q + 1)].rearrange("b c v -> c b v"))
             x0_tiles[i] = x0n
 
-        for g in range(2):
+        load_l(0)
+        for q in range(NVB):
             for h in range(2):
-                load_x2(2 * g, h)
-                load_x2(2 * g + 1, h)
-            if g == 0:
-                load_l(0)
+                load_x2(q, h)
+        load_x0(0)
         load_x1(0)
-        for i in range(4):
-            load_x0(i)
+        load_x0(1)
+        load_x0(2)
         load_l(1)
         load_x1(1)
+        for i in range(3, 6):
+            load_x0(i)
 
         w_codes = const.tile([P, OUT], U32, align_bytes=64)
         w_sc = const.tile([P, OUT], U8, align_bytes=64)
         bias_f = const.tile([P, 1], F32)
 
-        def prepare_weight():
+        def t_w():
             w_p = const.tile([P, C * K], BF16)
             nc.vector.tensor_copy(out=w_p[:].rearrange("p (k l u) -> p k l u", k=K, u=2),
                                   in_=w_nat[:].rearrange("p (u l k) -> p k l u", u=2, k=K))
@@ -111,8 +113,14 @@ def tile_graph_conv_pb_t_kernel(tc, x0, x1, x2, laplacian, weight, bias, out):
             w_ps = ps_t.tile([P, 2, P], F32, tag="tp")
             for h in range(2):
                 nc.tensor.transpose(w_ps[:, h, :], w_words[:, P * h:P * (h + 1)], ident[:])
+            return w_ps
+
+        def c_w(w_ps):
             wg = const.tile([P, OUT, 4], BF16, align_bytes=64)
             nc.scalar.copy(out=wg[:].bitcast(F32), in_=w_ps[:].rearrange("p h o -> p o h"))
+            return wg
+
+        def q_w(wg):
             nc.vector.quantize_mx(out=w_codes[:].bitcast(FP8X4), scales=w_sc[:],
                                   in_=wg[:].rearrange("p o t -> p (o t)"))
 
@@ -128,20 +136,19 @@ def tile_graph_conv_pb_t_kernel(tc, x0, x1, x2, laplacian, weight, bias, out):
 
         x2g = const.tile([P, 2, B, C, 4], BF16, align_bytes=64)
 
-        def regroup_x2(g):
-            src = x2n[:, g].rearrange("p u j (l b) -> p l (u j) b", b=B)
-            dst = x2g[:, g].rearrange("p b (l u) j -> p l (u j) b", u=2)
-            for n in range(UPB):
-                bs = slice(UB * n, UB * (n + 1))
-                if n < 2:
-                    nc.vector.tensor_copy(out=dst[:, :, :, bs], in_=src[:, :, :, bs])
-                else:
-                    nc.scalar.copy(out=dst[:, :, :, bs], in_=src[:, :, :, bs])
+        def regroup_x2(g, n):
+            bs = slice(UB * n, UB * (n + 1))
+            src = x2n[:, g].rearrange("p u j (l b) -> p l (u j) b", b=B)[:, :, :, bs]
+            dst = x2g[:, g, bs].rearrange("p b (l u) j -> p l (u j) b", u=2)
+            if n < V_RUNS:
+                nc.vector.tensor_copy(out=dst, in_=src)
+            else:
+                nc.scalar.copy(out=dst, in_=src)
 
-        def quant_x2(g, hq):
-            cs = slice(hq * 1024, (hq + 1) * 1024)
+        def quant_x2(g, n):
+            cs = slice(UB * C * n, UB * C * (n + 1))
             nc.vector.quantize_mx(out=x2_codes[:, g, cs].bitcast(FP8X4), scales=x2_sc[:, g, cs],
-                                  in_=x2g[:, g, 8 * hq:8 * hq + 8].rearrange("p b c j -> p (b c j)"))
+                                  in_=x2g[:, g, UB * n:UB * (n + 1)].rearrange("p b c j -> p (b c j)"))
 
         tl_tiles = {}
         ltg_tiles = {}
@@ -184,13 +191,20 @@ def tile_graph_conv_pb_t_kernel(tc, x0, x1, x2, laplacian, weight, bias, out):
         def gather(i, k, rows):
             r = i % UPB
             for e in range(2):
-                nc.vector.tensor_copy(
-                    out=feats[i][:, e, :, k, :].rearrange("p b (l u) -> p l u b", u=2),
-                    in_=rows[:, :, e, :].rearrange("p u (l b) -> p l u b", b=B)[:, :, :, UB * r:UB * (r + 1)])
+                dst = feats[i][:, e, :, k, :].rearrange("p b (l u) -> p l u b", u=2)
+                src = rows[:, :, e, :].rearrange("p u (l b) -> p l u b", b=B)[:, :, :, UB * r:UB * (r + 1)]
+                if i < V_FIRST:
+                    nc.vector.tensor_copy(out=dst, in_=src)
+                else:
+                    nc.gpsimd.tensor_scalar(out=dst.rearrange("p l u b -> p b l u"),
+                                            in0=src.rearrange("p l u b -> p b l u"),
+                                            scalar1=1.0, scalar2=0.0, op0=ALU.mult, op1=ALU.add)
 
-        def g_1(i):
+        def a_0(i):
             feat = feat_pool.tile([P, 2, UB, K, C], BF16, align_bytes=64)
             feats[i] = feat
+
+        def g_1(i):
             gather(i, 1, x1_tiles[i // UPB][:].rearrange("p e (u n) -> p u e n", u=2))
 
         def g_2(i):
@@ -210,18 +224,18 @@ def tile_graph_conv_pb_t_kernel(tc, x0, x1, x2, laplacian, weight, bias, out):
                            in_=x0_ps[i][:].rearrange("p e b c -> p (e b c)").bitcast(F32).rearrange(
                                "p (n l) -> p n l", l=HC))
 
-        def m_1(i):
+        def m_1(i, g):
             q, r = divmod(i, UPB)
             ns = slice(UB * C * r, UB * C * (r + 1))
             for e in range(2):
-                m1 = ps_1.tile([P, UB, C], F32, tag="m1")
-                m1s[(i, e)] = m1
+                if g == 0:
+                    m1 = ps_1.tile([P, UB, C], F32, tag="m1")
+                    m1s[(i, e)] = m1
                 vs = slice(VB * q + P * e, VB * q + P * (e + 1))
-                for g in range(2):
-                    nc.tensor.matmul_mx(out=m1[:].rearrange("p b c -> p (b c)"),
-                                        lhsT=lt_codes[:, g, vs].bitcast(FP8X4), lhsT_scale=lt_sc[:, g, vs],
-                                        rhs=x2_codes[:, g, ns].bitcast(FP8X4), rhs_scale=x2_sc[:, g, ns],
-                                        start=(g == 0), stop=(g == 1))
+                nc.tensor.matmul_mx(out=m1s[(i, e)][:].rearrange("p b c -> p (b c)"),
+                                    lhsT=lt_codes[:, g, vs].bitcast(FP8X4), lhsT_scale=lt_sc[:, g, vs],
+                                    rhs=x2_codes[:, g, ns].bitcast(FP8X4), rhs_scale=x2_sc[:, g, ns],
+                                    start=(g == 0), stop=(g == 1))
 
         def e_3(i):
             for e in range(2):
@@ -246,7 +260,7 @@ def tile_graph_conv_pb_t_kernel(tc, x0, x1, x2, laplacian, weight, bias, out):
 
         def c_f(i, b):
             src = f_ps[(i, b)][:].rearrange("p e h n -> p e n h")
-            if b < UB - 1:
+            if b < UB - 1 and not (i == NU - 1 and b == 1):
                 nc.scalar.copy(out=fg_tiles[i][:, b], in_=src)
             else:
                 nc.vector.tensor_copy(out=fg_tiles[i][:, b], in_=src)
@@ -255,8 +269,11 @@ def tile_graph_conv_pb_t_kernel(tc, x0, x1, x2, laplacian, weight, bias, out):
             f_codes = f_pool.tile([P, COLS], U32, align_bytes=64)
             f_sc = f_pool.tile([P, COLS], U8, align_bytes=64)
             codes[i] = (f_codes, f_sc)
-            nc.vector.quantize_mx(out=f_codes[:].bitcast(FP8X4), scales=f_sc[:],
-                                  in_=grouped[i][:].rearrange("p w t -> p (w t)"))
+            parts = 2 if i == NU - 1 else 1
+            for h in range(parts):
+                cs = slice(h * COLS // parts, (h + 1) * COLS // parts)
+                nc.vector.quantize_mx(out=f_codes[:, cs].bitcast(FP8X4), scales=f_sc[:, cs],
+                                      in_=grouped[i][:, cs, :].rearrange("p w t -> p (w t)"))
 
         def m_2(i):
             f_codes, f_sc = codes[i]
@@ -288,50 +305,88 @@ def tile_graph_conv_pb_t_kernel(tc, x0, x1, x2, laplacian, weight, bias, out):
             if 0 <= i < NU:
                 fn(i, *args)
 
-        regroup_x2(0)
-        quant_x2(0, 0)
         t_l(0, 0)
         t_l(0, 1)
+        w_ps = t_w()
         c_l(0, 0)
         c_l(0, 1)
         q_l(0)
-        regroup_x2(1)
-        quant_x2(1, 0)
+        wg = c_w(w_ps)
+        prepare_bias()
+        q_w(wg)
+        for n in range(UPB):
+            regroup_x2(0, n)
+        quant_x2(0, 0)
         quant_x2(0, 1)
+        for i in range(3):
+            a_0(i)
+        g_2(0)
+        m_1(0, 0)
+        t_0(0)
+        regroup_x2(1, 0)
+        quant_x2(1, 0)
+        regroup_x2(1, 2)
+        m_1(0, 1)
+        c_0(0)
+        regroup_x2(1, 1)
+        g_1(0)
+        g_1(1)
+        g_2(1)
+        regroup_x2(1, 3)
+        e_3(0)
+        quant_x2(1, 1)
+        t_0(1)
+        c_0(1)
+        t_f(0)
+        a_f(0)
+        for b in range(UB - 1):
+            c_f(0, b)
+        m_1(1, 0)
+        m_1(1, 1)
+        quant_x2(0, 2)
+        quant_x2(1, 2)
+        g_1(2)
+        g_2(2)
+        t_0(2)
+        c_0(2)
+        c_f(0, UB - 1)
+        e_3(1)
+        m_1(2, 0)
+        m_1(2, 1)
 
-        for i in range(-LEAD, NU + 1):
-            nq = (i + 6) // UPB
+        for i in range(NU):
+            nq = i // UPB + 1
             if i + X0_AHEAD < NU:
                 load_x0(i + X0_AHEAD)
-            if i == 0:
-                load_l(2)
             if i == 1:
                 load_x1(2)
-            if i == 4:
-                load_l(3)
+                load_l(2)
             if i == 5:
                 load_x1(3)
-            emit(f_o, i - 1)
+                load_l(3)
+            emit(a_0, i + 3)
+            emit(g_1, i + 3)
+            emit(g_2, i + 3)
             emit(t_f, i + 1)
-            emit(e_3, i + 2)
+            emit(q_f, i)
             emit(a_f, i + 1)
             for b in range(UB - 1):
                 emit(c_f, i + 1, b)
-            emit(q_f, i)
+            emit(e_3, i + 2)
             emit(c_f, i + 1, UB - 1)
-            emit(g_1, i + 3)
             emit(t_0, i + 3)
-            if (i + 6) % UPB < 2 and 1 <= nq < NVB:
-                t_l(nq, (i + 6) % UPB)
-                c_l(nq, (i + 6) % UPB)
             emit(c_0, i + 3)
-            if (i + 6) % UPB == 2 and 1 <= nq < NVB:
-                q_l(nq)
-            if i == -3:
-                quant_x2(1, 1)
-            if i == -1:
-                prepare_weight()
-                prepare_bias()
-            emit(g_2, i + 3)
-            emit(m_1, i + 3)
+            if i == 0:
+                quant_x2(0, 3)
+                quant_x2(1, 3)
+            if nq < NVB:
+                if i % UPB == 0:
+                    t_l(nq, 0)
+                    t_l(nq, 1)
+                    c_l(nq, 0)
+                    c_l(nq, 1)
+                    q_l(nq)
             emit(m_2, i)
+            emit(f_o, i)
+            emit(m_1, i + 3, 0)
+            emit(m_1, i + 3, 1)

@@ -24,7 +24,6 @@ FLOPS = 2 * V * V * C * B + 2 * B * V * C * K * OUT
 
 X0_AHEAD = 6
 V_RUNS = 2
-V_FIRST = 1
 
 
 def tile_graph_conv_pb_t_kernel(tc, x0, x1, x2, laplacian, weight, bias, out):
@@ -191,14 +190,9 @@ def tile_graph_conv_pb_t_kernel(tc, x0, x1, x2, laplacian, weight, bias, out):
         def gather(i, k, rows):
             r = i % UPB
             for e in range(2):
-                dst = feats[i][:, e, :, k, :].rearrange("p b (l u) -> p l u b", u=2)
-                src = rows[:, :, e, :].rearrange("p u (l b) -> p l u b", b=B)[:, :, :, UB * r:UB * (r + 1)]
-                if i < V_FIRST:
-                    nc.vector.tensor_copy(out=dst, in_=src)
-                else:
-                    nc.gpsimd.tensor_scalar(out=dst.rearrange("p l u b -> p b l u"),
-                                            in0=src.rearrange("p l u b -> p b l u"),
-                                            scalar1=1.0, scalar2=0.0, op0=ALU.mult, op1=ALU.add)
+                nc.vector.tensor_copy(
+                    out=feats[i][:, e, :, k, :].rearrange("p b (l u) -> p l u b", u=2),
+                    in_=rows[:, :, e, :].rearrange("p u (l b) -> p l u b", b=B)[:, :, :, UB * r:UB * (r + 1)])
 
         def a_0(i):
             feat = feat_pool.tile([P, 2, UB, K, C], BF16, align_bytes=64)
@@ -260,7 +254,7 @@ def tile_graph_conv_pb_t_kernel(tc, x0, x1, x2, laplacian, weight, bias, out):
 
         def c_f(i, b):
             src = f_ps[(i, b)][:].rearrange("p e h n -> p e n h")
-            if b < UB - 1 and not (i == NU - 1 and b == 1):
+            if b < UB - 1 or i % UPB:
                 nc.scalar.copy(out=fg_tiles[i][:, b], in_=src)
             else:
                 nc.vector.tensor_copy(out=fg_tiles[i][:, b], in_=src)
@@ -330,11 +324,10 @@ def tile_graph_conv_pb_t_kernel(tc, x0, x1, x2, laplacian, weight, bias, out):
         c_0(0)
         regroup_x2(1, 1)
         g_1(0)
-        g_1(1)
-        g_2(1)
         regroup_x2(1, 3)
-        e_3(0)
         quant_x2(1, 1)
+        e_3(0)
+        g_1(1)
         t_0(1)
         c_0(1)
         t_f(0)
@@ -343,14 +336,15 @@ def tile_graph_conv_pb_t_kernel(tc, x0, x1, x2, laplacian, weight, bias, out):
             c_f(0, b)
         m_1(1, 0)
         m_1(1, 1)
+        g_2(1)
         quant_x2(0, 2)
         quant_x2(1, 2)
-        g_1(2)
-        g_2(2)
         t_0(2)
         c_0(2)
         c_f(0, UB - 1)
         e_3(1)
+        g_1(2)
+        g_2(2)
         m_1(2, 0)
         m_1(2, 1)
 
@@ -365,8 +359,6 @@ def tile_graph_conv_pb_t_kernel(tc, x0, x1, x2, laplacian, weight, bias, out):
                 load_x1(3)
                 load_l(3)
             emit(a_0, i + 3)
-            emit(g_1, i + 3)
-            emit(g_2, i + 3)
             emit(t_f, i + 1)
             emit(q_f, i)
             emit(a_f, i + 1)
@@ -374,6 +366,8 @@ def tile_graph_conv_pb_t_kernel(tc, x0, x1, x2, laplacian, weight, bias, out):
                 emit(c_f, i + 1, b)
             emit(e_3, i + 2)
             emit(c_f, i + 1, UB - 1)
+            emit(g_1, i + 3)
+            emit(g_2, i + 3)
             emit(t_0, i + 3)
             emit(c_0, i + 3)
             if i == 0:

@@ -37,8 +37,7 @@ def tile_graph_conv_pb_t_kernel(tc, x0, x1, x2, laplacian, weight, bias, out):
         f_pool = ctx.enter_context(tc.tile_pool(name="fp", bufs=3))
         o_pool = ctx.enter_context(tc.tile_pool(name="op", bufs=3))
         ps_t = ctx.enter_context(tc.psum_pool(name="pst", bufs=4))
-        ps_1 = ctx.enter_context(tc.psum_pool(name="ps1", bufs=2))
-        ps_2 = ctx.enter_context(tc.psum_pool(name="ps2", bufs=2))
+        ps_m = ctx.enter_context(tc.psum_pool(name="psm", bufs=4))
         ctx.enter_context(tc.manual_schedule())
 
         ident = const.tile([P, P], F32)
@@ -223,7 +222,7 @@ def tile_graph_conv_pb_t_kernel(tc, x0, x1, x2, laplacian, weight, bias, out):
             ns = slice(UB * C * r, UB * C * (r + 1))
             for e in range(2):
                 if g == 0:
-                    m1 = ps_1.tile([P, UB, C], F32, tag="m1")
+                    m1 = ps_m.tile([P, UB, C], F32, tag="m")
                     m1s[(i, e)] = m1
                 vs = slice(VB * q + P * e, VB * q + P * (e + 1))
                 nc.tensor.matmul_mx(out=m1s[(i, e)][:].rearrange("p b c -> p (b c)"),
@@ -254,7 +253,7 @@ def tile_graph_conv_pb_t_kernel(tc, x0, x1, x2, laplacian, weight, bias, out):
 
         def c_f(i, b):
             src = f_ps[(i, b)][:].rearrange("p e h n -> p e n h")
-            if b < UB - 1 or i % UPB:
+            if b < UB - 1 or i % 2 or i == 0:
                 nc.scalar.copy(out=fg_tiles[i][:, b], in_=src)
             else:
                 nc.vector.tensor_copy(out=fg_tiles[i][:, b], in_=src)
@@ -273,7 +272,7 @@ def tile_graph_conv_pb_t_kernel(tc, x0, x1, x2, laplacian, weight, bias, out):
             f_codes, f_sc = codes[i]
             for l in range(2):
                 cs = slice(l * 512, (l + 1) * 512)
-                m2 = ps_2.tile([P, 512], F32, tag="m2")
+                m2 = ps_m.tile([P, 512], F32, tag="m")
                 m2s[(i, l)] = m2
                 nc.tensor.matmul_mx(out=m2[:], lhsT=w_codes[:].bitcast(FP8X4), lhsT_scale=w_sc[:],
                                     rhs=f_codes[:, cs].bitcast(FP8X4), rhs_scale=f_sc[:, cs],
@@ -315,7 +314,9 @@ def tile_graph_conv_pb_t_kernel(tc, x0, x1, x2, laplacian, weight, bias, out):
         for i in range(3):
             a_0(i)
         g_2(0)
+        g_2(1)
         m_1(0, 0)
+        m_1(1, 0)
         t_0(0)
         regroup_x2(1, 0)
         quant_x2(1, 0)
@@ -323,26 +324,23 @@ def tile_graph_conv_pb_t_kernel(tc, x0, x1, x2, laplacian, weight, bias, out):
         m_1(0, 1)
         c_0(0)
         regroup_x2(1, 1)
+        quant_x2(1, 1)
+        m_1(1, 1)
         g_1(0)
         regroup_x2(1, 3)
-        quant_x2(1, 1)
         e_3(0)
-        g_1(1)
-        t_0(1)
-        c_0(1)
         t_f(0)
         a_f(0)
-        for b in range(UB - 1):
+        for b in range(UB):
             c_f(0, b)
-        m_1(1, 0)
-        m_1(1, 1)
-        g_2(1)
-        quant_x2(0, 2)
-        quant_x2(1, 2)
+        g_1(1)
+        e_3(1)
+        t_0(1)
+        c_0(1)
         t_0(2)
         c_0(2)
-        c_f(0, UB - 1)
-        e_3(1)
+        quant_x2(0, 2)
+        quant_x2(1, 2)
         g_1(2)
         g_2(2)
         m_1(2, 0)

@@ -58,16 +58,15 @@ def tile_graph_conv_pb_t_kernel(tc, x0, x1, x2, laplacian, weight, bias, out):
         nc.vector.memset(bias_rows[:], 0.0)
         nc.scalar.dma_start(out=bias_rows[0:1, :], in_=bias.rearrange("(r o) -> r o", r=1))
 
-        x2n = const.tile([P, 2, 2, 4, HC * B], BF16)
+        x2n = const.tile([P, 2, 4, C * B], BF16)
         l_tiles = {}
         x1_tiles = {}
         x0_tiles = {}
 
-        def load_x2(q, h):
+        def load_x2(q):
             g, s = divmod(q, 2)
-            ns = slice(1024 * h, 1024 * (h + 1))
-            nc.sync.dma_start(out=x2n[:, g, h, 2 * s:2 * s + 2, :],
-                              in_=x2[VB * q:VB * (q + 1), ns].rearrange("(p e) n -> p e n", e=2))
+            nc.sync.dma_start(out=x2n[:, g, 2 * s:2 * s + 2, :],
+                              in_=x2[VB * q:VB * (q + 1), :].rearrange("(p e) n -> p e n", e=2))
 
         def load_l(q):
             l_nat = chunk.tile([P, 2, V], BF16)
@@ -88,8 +87,7 @@ def tile_graph_conv_pb_t_kernel(tc, x0, x1, x2, laplacian, weight, bias, out):
 
         load_l(0)
         for q in range(NVB):
-            for h in range(2):
-                load_x2(q, h)
+            load_x2(q)
         load_x0(0)
         load_x1(0)
         load_x0(1)
@@ -136,8 +134,8 @@ def tile_graph_conv_pb_t_kernel(tc, x0, x1, x2, laplacian, weight, bias, out):
 
         def regroup_x2(g, n):
             bs = slice(UB * n, UB * (n + 1))
-            src = x2n[:, g].rearrange("p u j (l b) -> p l (u j) b", b=B)[:, :, :, bs]
-            dst = x2g[:, g, bs].rearrange("p b (l u) j -> p l (u j) b", u=2)
+            src = x2n[:, g].rearrange("p j (u l b) -> p l u j b", u=2, b=B)[:, :, :, :, bs]
+            dst = x2g[:, g, bs].rearrange("p b (l u) j -> p l u j b", u=2)
             if n < V_RUNS:
                 nc.vector.tensor_copy(out=dst, in_=src)
             else:
@@ -188,21 +186,20 @@ def tile_graph_conv_pb_t_kernel(tc, x0, x1, x2, laplacian, weight, bias, out):
 
         def gather(i, k, rows):
             r = i % UPB
-            for e in range(2):
-                nc.vector.tensor_copy(
-                    out=feats[i][:, e, :, k, :].rearrange("p b (l u) -> p l u b", u=2),
-                    in_=rows[:, :, e, :].rearrange("p u (l b) -> p l u b", b=B)[:, :, :, UB * r:UB * (r + 1)])
+            nc.vector.tensor_copy(
+                out=feats[i][:, :, :, k, :].rearrange("p e b (l u) -> p e l u b", u=2),
+                in_=rows.rearrange("p e (u l b) -> p e l u b", u=2, b=B)[:, :, :, :, UB * r:UB * (r + 1)])
 
         def a_0(i):
             feat = feat_pool.tile([P, 2, UB, K, C], BF16, align_bytes=64)
             feats[i] = feat
 
         def g_1(i):
-            gather(i, 1, x1_tiles[i // UPB][:].rearrange("p e (u n) -> p u e n", u=2))
+            gather(i, 1, x1_tiles[i // UPB][:])
 
         def g_2(i):
             g, s = divmod(i // UPB, 2)
-            gather(i, 2, x2n[:, g, :, 2 * s:2 * s + 2, :])
+            gather(i, 2, x2n[:, g, 2 * s:2 * s + 2, :])
 
         def t_0(i):
             tp = ps_t.tile([P, 2, UB, C], BF16, tag="tp")
@@ -235,9 +232,9 @@ def tile_graph_conv_pb_t_kernel(tc, x0, x1, x2, laplacian, weight, bias, out):
                 nc.vector.scalar_tensor_tensor(out=feats[i][:, e, :, 3, :], in0=m1s[(i, e)][:], scalar=2.0,
                                                in1=feats[i][:, e, :, 1, :], op0=ALU.mult, op1=ALU.subtract)
 
-        def t_f(i):
+        def t_f(i, b_range):
             words = feat_words(i)
-            for b in range(UB):
+            for b in b_range:
                 tp = ps_t.tile([P, 2, 2, P], F32, tag="tp")
                 f_ps[(i, b)] = tp
                 for e in range(2):
@@ -253,7 +250,7 @@ def tile_graph_conv_pb_t_kernel(tc, x0, x1, x2, laplacian, weight, bias, out):
 
         def c_f(i, b):
             src = f_ps[(i, b)][:].rearrange("p e h n -> p e n h")
-            if b < UB - 1 or i % 2 or i == 0:
+            if b < UB - 1 or (i % 2 and i < NU - 1) or i == 0:
                 nc.scalar.copy(out=fg_tiles[i][:, b], in_=src)
             else:
                 nc.vector.tensor_copy(out=fg_tiles[i][:, b], in_=src)
@@ -324,12 +321,13 @@ def tile_graph_conv_pb_t_kernel(tc, x0, x1, x2, laplacian, weight, bias, out):
         m_1(0, 1)
         c_0(0)
         regroup_x2(1, 1)
-        quant_x2(1, 1)
-        m_1(1, 1)
         g_1(0)
         regroup_x2(1, 3)
         e_3(0)
-        t_f(0)
+        quant_x2(1, 1)
+        t_f(0, range(2))
+        m_1(1, 1)
+        t_f(0, range(2, UB))
         a_f(0)
         for b in range(UB):
             c_f(0, b)
@@ -357,7 +355,7 @@ def tile_graph_conv_pb_t_kernel(tc, x0, x1, x2, laplacian, weight, bias, out):
                 load_x1(3)
                 load_l(3)
             emit(a_0, i + 3)
-            emit(t_f, i + 1)
+            emit(t_f, i + 1, range(UB))
             emit(q_f, i)
             emit(a_f, i + 1)
             for b in range(UB - 1):

@@ -48,15 +48,15 @@ def tile_graph_conv_pb_t_kernel(tc, x0, x1, x2, laplacian, weight, bias, out):
         nc.gpsimd.tensor_copy(out=perm[:].rearrange("p (l u) -> p l u", u=2),
                               in_=ident_bf[:].rearrange("p (u l) -> p l u", u=2))
 
-        warm = const.tile([P, 2], F32)
-        nc.vector.memset(warm[:], 0.0)
-        nc.scalar.activation(out=warm[:, 0:1], in_=warm[:, 1:2], func=ACT.Identity, scale=1.0)
-
         w_nat = const.tile([P, C * K], BF16)
         nc.scalar.dma_start(out=w_nat[:], in_=weight)
         bias_rows = const.tile([P, P], BF16)
         nc.vector.memset(bias_rows[:], 0.0)
         nc.scalar.dma_start(out=bias_rows[0:1, :], in_=bias.rearrange("(r o) -> r o", r=1))
+
+        warm = const.tile([P, 2], F32)
+        nc.vector.memset(warm[:], 0.0)
+        nc.scalar.activation(out=warm[:, 0:1], in_=warm[:, 1:2], func=ACT.Identity, scale=1.0)
 
         x2n = const.tile([P, 2, 4, C * B], BF16)
         l_tiles = {}
@@ -302,12 +302,12 @@ def tile_graph_conv_pb_t_kernel(tc, x0, x1, x2, laplacian, weight, bias, out):
         c_l(0, 1)
         q_l(0)
         wg = c_w(w_ps)
-        prepare_bias()
         q_w(wg)
         for n in range(UPB):
             regroup_x2(0, n)
         quant_x2(0, 0)
         quant_x2(0, 1)
+        prepare_bias()
         for i in range(3):
             a_0(i)
         g_2(0)

from contextlib import ExitStack

import concourse.mybir as mybir
from concourse.masks import make_identity

F32 = mybir.dt.float32
BF16 = mybir.dt.bfloat16
U32 = mybir.dt.uint32
U8 = mybir.dt.uint8
FP8X4 = mybir.dt.float8_e4m3fn_x4
ALU = mybir.AluOpType
ACT = mybir.ActivationFunctionType

P = 128
B, C, V, K, OUT = 16, 128, 1024, 4, 128
HC = C // 2
VB = 256
NVB = V // VB
UB = 4
UPB = B // UB
NU = NVB * UPB
COLS = UB * VB
FLOPS = 2 * V * V * C * B + 2 * B * V * C * K * OUT

X0_AHEAD = 6
V_RUNS = 2


def tile_graph_conv_pb_t_kernel(tc, x0, x1, x2, laplacian, weight, bias, out):
    nc = tc.nc
    with ExitStack() as ctx:
        const = ctx.enter_context(tc.tile_pool(name="const", bufs=1))
        chunk = ctx.enter_context(tc.tile_pool(name="chunk", bufs=2))
        x0_pool = ctx.enter_context(tc.tile_pool(name="x0p", bufs=6))
        feat_pool = ctx.enter_context(tc.tile_pool(name="featp", bufs=4))
        grouped_pool = ctx.enter_context(tc.tile_pool(name="groupedp", bufs=2))
        f_pool = ctx.enter_context(tc.tile_pool(name="fp", bufs=3))
        o_pool = ctx.enter_context(tc.tile_pool(name="op", bufs=3))
        ps_t = ctx.enter_context(tc.psum_pool(name="pst", bufs=4))
        ps_m = ctx.enter_context(tc.psum_pool(name="psm", bufs=4))
        ctx.enter_context(tc.manual_schedule())

        ident = const.tile([P, P], F32)
        make_identity(nc, ident[:])
        ident_bf = const.tile([P, P], BF16)
        make_identity(nc, ident_bf[:])
        perm = const.tile([P, P], BF16)
        nc.gpsimd.tensor_copy(out=perm[:].rearrange("p (l u) -> p l u", u=2),
                              in_=ident_bf[:].rearrange("p (u l) -> p l u", u=2))

        w_nat = const.tile([P, C * K], BF16)
        nc.scalar.dma_start(out=w_nat[:], in_=weight)
        bias_rows = const.tile([P, P], BF16)
        nc.vector.memset(bias_rows[:], 0.0)
        nc.scalar.dma_start(out=bias_rows[0:1, :], in_=bias.rearrange("(r o) -> r o", r=1))

        warm = const.tile([P, 2], F32)
        nc.vector.memset(warm[:], 0.0)
        nc.scalar.activation(out=warm[:, 0:1], in_=warm[:, 1:2], func=ACT.Identity, scale=1.0)

        x2n = const.tile([P, 2, 4, C * B], BF16)
        l_tiles = {}
        x1_tiles = {}
        x0_tiles = {}

        def load_x2(q):
            g, s = divmod(q, 2)
            nc.sync.dma_start(out=x2n[:, g, 2 * s:2 * s + 2, :],
                              in_=x2[VB * q:VB * (q + 1), :].rearrange("(p e) n -> p e n", e=2))

        def load_l(q):
            l_nat = chunk.tile([P, 2, V], BF16)
            nc.sync.dma_start(out=l_nat[:], in_=laplacian[VB * q:VB * (q + 1), :].rearrange("(p e) u -> p e u", e=2))
            l_tiles[q] = l_nat

        def load_x1(q):
            x1c = chunk.tile([P, 2, C * B], BF16)
            nc.sync.dma_start(out=x1c[:], in_=x1[VB * q:VB * (q + 1), :].rearrange("(p e) n -> p e n", e=2))
            x1_tiles[q] = x1c

        def load_x0(i):
            q, r = divmod(i, UPB)
            x0n = x0_pool.tile([P, UB, VB], BF16)
            nc.sync.dma_start(out=x0n[:],
                              in_=x0[UB * r:UB * (r + 1), :, VB * q:VB * (q + 1)].rearrange("b c v -> c b v"))
            x0_tiles[i] = x0n

        load_l(0)
        for q in range(NVB):
            load_x2(q)
        load_x0(0)
        load_x1(0)
        load_x0(1)
        load_x0(2)
        load_l(1)
        load_x1(1)
        for i in range(3, 6):
            load_x0(i)

        w_codes = const.tile([P, OUT], U32, align_bytes=64)
        w_sc = const.tile([P, OUT], U8, align_bytes=64)
        bias_f = const.tile([P, 1], F32)

        def t_w():
            w_p = const.tile([P, C * K], BF16)
            nc.vector.tensor_copy(out=w_p[:].rearrange("p (k l u) -> p k l u", k=K, u=2),
                                  in_=w_nat[:].rearrange("p (u l k) -> p k l u", u=2, k=K))
            w_words = w_p[:].bitcast(F32)
            w_ps = ps_t.tile([P, 2, P], F32, tag="tp")
            for h in range(2):
                nc.tensor.transpose(w_ps[:, h, :], w_words[:, P * h:P * (h + 1)], ident[:])
            return w_ps

        def c_w(w_ps):
            wg = const.tile([P, OUT, 4], BF16, align_bytes=64)
            nc.scalar.copy(out=wg[:].bitcast(F32), in_=w_ps[:].rearrange("p h o -> p o h"))
            return wg

        def q_w(wg):
            nc.vector.quantize_mx(out=w_codes[:].bitcast(FP8X4), scales=w_sc[:],
                                  in_=wg[:].rearrange("p o t -> p (o t)"))

        def prepare_bias():
            b_ps = ps_t.tile([P, P], BF16, tag="tp")
            nc.tensor.transpose(b_ps[:], bias_rows[:], ident_bf[:])
            nc.vector.tensor_copy(out=bias_f[:], in_=b_ps[:, 0:1])

        x2_codes = const.tile([P, 2, B * C], U32, align_bytes=64)
        x2_sc = const.tile([P, 2, B * C], U8, align_bytes=64)
        lt_codes = const.tile([P, 2, V], U32, align_bytes=64)
        lt_sc = const.tile([P, 2, V], U8, align_bytes=64)

        x2g = const.tile([P, 2, B, C, 4], BF16, align_bytes=64)

        def regroup_x2(g, n):
            bs = slice(UB * n, UB * (n + 1))
            src = x2n[:, g].rearrange("p j (u l b) -> p l u j b", u=2, b=B)[:, :, :, :, bs]
            dst = x2g[:, g, bs].rearrange("p b (l u) j -> p l u j b", u=2)
            if n < V_RUNS:
                nc.vector.tensor_copy(out=dst, in_=src)
            else:
                nc.scalar.copy(out=dst, in_=src)

        def quant_x2(g, n):
            cs = slice(UB * C * n, UB * C * (n + 1))
            nc.vector.quantize_mx(out=x2_codes[:, g, cs].bitcast(FP8X4), scales=x2_sc[:, g, cs],
                                  in_=x2g[:, g, UB * n:UB * (n + 1)].rearrange("p b c j -> p (b c j)"))

        tl_tiles = {}
        ltg_tiles = {}

        def t_l(q, g):
            l_words = l_tiles[q][:].bitcast(F32)
            tp = ps_t.tile([P, 2, VB], F32, tag="tp")
            tl_tiles[(q, g)] = tp
            for s in range(2):
                for e in range(2):
                    nc.tensor.transpose(tp[:, s, e * P:(e + 1) * P],
                                        l_words[:, e, 256 * g + 128 * s:256 * g + 128 * (s + 1)], ident[:])

        def c_l(q, g):
            if g == 0:
                ltg = chunk.tile([P, 2, VB, 4], BF16, align_bytes=64)
                ltg_tiles[q] = ltg
            ltg_words = ltg_tiles[q][:].bitcast(F32)
            nc.scalar.copy(out=ltg_words[:, g, :, :], in_=tl_tiles[(q, g)][:].rearrange("p s v -> p v s"))

        def q_l(q):
            vs = slice(q * VB, (q + 1) * VB)
            for g in range(2):
                nc.vector.quantize_mx(out=lt_codes[:, g, vs].bitcast(FP8X4), scales=lt_sc[:, g, vs],
                                      in_=ltg_tiles[q][:, g, :, :].rearrange("p v t -> p (v t)"))

        feats = {}
        x0_ps = {}
        f_ps = {}
        m1s = {}
        m2s = {}
        grouped = {}
        fg_tiles = {}
        codes = {}

        def feat_words(i):
            return feats[i][:].rearrange("p e b k c -> p (e b k c)").bitcast(F32).rearrange(
                "p (e b w) -> p e b w", e=2, b=UB)

        def gather(i, k, rows):
            r = i % UPB
            nc.vector.tensor_copy(
                out=feats[i][:, :, :, k, :].rearrange("p e b (l u) -> p e l u b", u=2),
                in_=rows.rearrange("p e (u l b) -> p e l u b", u=2, b=B)[:, :, :, :, UB * r:UB * (r + 1)])

        def a_0(i):
            feat = feat_pool.tile([P, 2, UB, K, C], BF16, align_bytes=64)
            feats[i] = feat

        def g_1(i):
            gather(i, 1, x1_tiles[i // UPB][:])

        def g_2(i):
            g, s = divmod(i // UPB, 2)
            gather(i, 2, x2n[:, g, 2 * s:2 * s + 2, :])

        def t_0(i):
            tp = ps_t.tile([P, 2, UB, C], BF16, tag="tp")
            x0_ps[i] = tp
            for e in range(2):
                for b in range(UB):
                    nc.tensor.transpose(tp[:, e, b, :], x0_tiles[i][:, b, e:VB:2], perm[:])

        def c_0(i):
            words = feat_words(i).rearrange("p e b (k l) -> p (e b) k l", k=K)
            nc.scalar.copy(out=words[:, :, 0, :],
                           in_=x0_ps[i][:].rearrange("p e b c -> p (e b c)").bitcast(F32).rearrange(
                               "p (n l) -> p n l", l=HC))

        def m_1(i, g):
            q, r = divmod(i, UPB)
            ns = slice(UB * C * r, UB * C * (r + 1))
            for e in range(2):
                if g == 0:
                    m1 = ps_m.tile([P, UB, C], F32, tag="m")
                    m1s[(i, e)] = m1
                vs = slice(VB * q + P * e, VB * q + P * (e + 1))
                nc.tensor.matmul_mx(out=m1s[(i, e)][:].rearrange("p b c -> p (b c)"),
                                    lhsT=lt_codes[:, g, vs].bitcast(FP8X4), lhsT_scale=lt_sc[:, g, vs],
                                    rhs=x2_codes[:, g, ns].bitcast(FP8X4), rhs_scale=x2_sc[:, g, ns],
                                    start=(g == 0), stop=(g == 1))

        def e_3(i):
            for e in range(2):
                nc.vector.scalar_tensor_tensor(out=feats[i][:, e, :, 3, :], in0=m1s[(i, e)][:], scalar=2.0,
                                               in1=feats[i][:, e, :, 1, :], op0=ALU.mult, op1=ALU.subtract)

        def t_f(i, b_range):
            words = feat_words(i)
            for b in b_range:
                tp = ps_t.tile([P, 2, 2, P], F32, tag="tp")
                f_ps[(i, b)] = tp
                for e in range(2):
                    for h in range(2):
                        nc.tensor.transpose(tp[:, e, h, :], words[:, e, b, P * h:P * (h + 1)], ident[:])

        def a_f(i):
            fg = grouped_pool.tile([P, COLS, K], BF16, align_bytes=64)
            grouped[i] = fg
            fg_words = fg[:].rearrange("p w t -> p (w t)").bitcast(F32).rearrange(
                "p (b e n h) -> p b e n h", b=UB, e=2, h=2)
            fg_tiles[i] = fg_words

        def c_f(i, b):
            src = f_ps[(i, b)][:].rearrange("p e h n -> p e n h")
            if b < UB - 1 or (i % 2 and i < NU - 1) or i == 0:
                nc.scalar.copy(out=fg_tiles[i][:, b], in_=src)
            else:
                nc.vector.tensor_copy(out=fg_tiles[i][:, b], in_=src)

        def q_f(i):
            f_codes = f_pool.tile([P, COLS], U32, align_bytes=64)
            f_sc = f_pool.tile([P, COLS], U8, align_bytes=64)
            codes[i] = (f_codes, f_sc)
            parts = 2 if i == NU - 1 else 1
            for h in range(parts):
                cs = slice(h * COLS // parts, (h + 1) * COLS // parts)
                nc.vector.quantize_mx(out=f_codes[:, cs].bitcast(FP8X4), scales=f_sc[:, cs],
                                      in_=grouped[i][:, cs, :].rearrange("p w t -> p (w t)"))

        def m_2(i):
            f_codes, f_sc = codes[i]
            for l in range(2):
                cs = slice(l * 512, (l + 1) * 512)
                m2 = ps_m.tile([P, 512], F32, tag="m")
                m2s[(i, l)] = m2
                nc.tensor.matmul_mx(out=m2[:], lhsT=w_codes[:].bitcast(FP8X4), lhsT_scale=w_sc[:],
                                    rhs=f_codes[:, cs].bitcast(FP8X4), rhs_scale=f_sc[:, cs],
                                    start=True, stop=True)

        def f_o(i):
            q, r = divmod(i, UPB)
            o_sb = o_pool.tile([P, UB, VB], F32)
            dst = out[UB * r:UB * (r + 1), :, VB * q:VB * (q + 1)].rearrange("b o v -> o b v")
            for l in range(2):
                src = m2s[(i, l)][:].rearrange("p (b e n) -> p b n e", b=2, e=2)
                osl = o_sb[:, 2 * l:2 * l + 2, :].rearrange("p b (n e) -> p b n e", e=2)
                if i == NU - 1 and l == 1:
                    nc.vector.tensor_scalar(out=osl, in0=src, scalar1=bias_f[:, 0:1], scalar2=None, op0=ALU.add)
                else:
                    nc.scalar.activation(out=osl, in_=src, func=ACT.Identity, bias=bias_f[:, 0:1], scale=1.0)
                if i == NU - 1:
                    nc.sync.dma_start(out=dst[:, 2 * l:2 * l + 2, :], in_=o_sb[:, 2 * l:2 * l + 2, :])
            if i < NU - 1:
                nc.sync.dma_start(out=dst, in_=o_sb[:])

        def emit(fn, i, *args):
            if 0 <= i < NU:
                fn(i, *args)

        t_l(0, 0)
        t_l(0, 1)
        w_ps = t_w()
        c_l(0, 0)
        c_l(0, 1)
        q_l(0)
        wg = c_w(w_ps)
        q_w(wg)
        for n in range(UPB):
            regroup_x2(0, n)
        quant_x2(0, 0)
        quant_x2(0, 1)
        prepare_bias()
        for i in range(3):
            a_0(i)
        g_2(0)
        g_2(1)
        m_1(0, 0)
        m_1(1, 0)
        t_0(0)
        regroup_x2(1, 0)
        quant_x2(1, 0)
        regroup_x2(1, 2)
        m_1(0, 1)
        c_0(0)
        regroup_x2(1, 1)
        g_1(0)
        regroup_x2(1, 3)
        e_3(0)
        quant_x2(1, 1)
        t_f(0, range(2))
        m_1(1, 1)
        t_f(0, range(2, UB))
        a_f(0)
        for b in range(UB):
            c_f(0, b)
        g_1(1)
        e_3(1)
        t_0(1)
        c_0(1)
        t_0(2)
        c_0(2)
        quant_x2(0, 2)
        quant_x2(1, 2)
        g_1(2)
        g_2(2)
        m_1(2, 0)
        m_1(2, 1)

        for i in range(NU):
            nq = i // UPB + 1
            if i + X0_AHEAD < NU:
                load_x0(i + X0_AHEAD)
            if i == 1:
                load_x1(2)
                load_l(2)
            if i == 5:
                load_x1(3)
                load_l(3)
            emit(a_0, i + 3)
            emit(t_f, i + 1, range(UB))
            emit(q_f, i)
            emit(a_f, i + 1)
            for b in range(UB - 1):
                emit(c_f, i + 1, b)
            emit(e_3, i + 2)
            emit(c_f, i + 1, UB - 1)
            emit(g_1, i + 3)
            emit(g_2, i + 3)
            emit(t_0, i + 3)
            emit(c_0, i + 3)
            if i == 0:
                quant_x2(0, 3)
                quant_x2(1, 3)
            if nq < NVB:
                if i % UPB == 0:
                    t_l(nq, 0)
                    t_l(nq, 1)
                    c_l(nq, 0)
                    c_l(nq, 1)
                    q_l(nq)
            emit(m_2, i)
            emit(f_o, i)
            emit(m_1, i + 3, 0)
            emit(m_1, i + 3, 1)
